import numpy as np
import ml_dtypes


def mxq(x, axis, fmt="e4m3"):
    dtype, down = {"e4m3": (ml_dtypes.float8_e4m3fn, 7), "e5m2": (ml_dtypes.float8_e5m2, 14)}[fmt]
    v = np.moveaxis(np.asarray(x, np.float32).astype(ml_dtypes.bfloat16).astype(np.float64), axis, -1)
    blocks = v.reshape(v.shape[:-1] + (-1, 32))
    amax = np.abs(blocks).max(-1, keepdims=True)
    byte = np.maximum(np.where(amax > 0, np.frexp(amax)[1] - 1 + 127, 0) - down, 1)
    scale = np.exp2(byte - 127.0)
    codes = (blocks / scale).astype(np.float32).astype(dtype).astype(np.float64)
    return np.moveaxis((codes * scale).reshape(v.shape), -1, axis)


WIDE = False


def mx_kscale(k):
    if not WIDE:
        return np.ones(k)
    levels = np.array([10, -10, 5, -5, 0])
    if k % 512:
        return np.exp2(np.random.permutation(np.resize(levels, k // 32))).repeat(32)
    a = np.empty((k // 512, 16))
    for p in range(k // 512):
        a[p, :8] = np.random.permutation(np.resize(levels, 8))
        for g in range(8):
            far = levels[np.abs(levels - a[p, g]) >= 10]
            a[p, g + 8] = far[np.random.randint(len(far))]
    return np.exp2(a.ravel()).repeat(32)


BF16 = ml_dtypes.bfloat16


def bf(x):
    return np.asarray(x, np.float32).astype(BF16)


def f64(x):
    return np.asarray(x).astype(np.float64)


T, B, D_IN, D_H, D_K, D_OUT = 8, 256, 512, 1024, 1024, 256


def setup_inputs():
    s, t = mx_kscale(D_H), mx_kscale(D_K)
    return {"h1": bf(np.maximum(np.random.standard_normal((T, B, D_H)), 0.0) * s),
            "W2": bf(np.random.standard_normal((T, D_H, D_K)) * 1.4 / np.sqrt(D_H) / s[:, None] * t),
            "b2": bf(np.random.standard_normal((T, D_K)) * 0.2 * t),
            "W3": bf(np.random.standard_normal((T, D_K, D_OUT)) * 1.4 / np.sqrt(D_K) / t[:, None]),
            "b3": bf(np.random.standard_normal((T, D_OUT)) * 0.2)}


def reference(h1, W2, b2, W3, b3):
    h2 = np.maximum((mxq(f64(h1), 2, "e4m3") @ mxq(f64(W2), 1, "e4m3")) + f64(b2)[:, None, :], 0.0)
    out = (mxq(h2, 2, "e4m3") @ mxq(f64(W3), 1, "e4m3")) + f64(b3)[:, None, :]
    return out.mean(axis=0)

@@ -1,0 +1,328 @@
+from contextlib import ExitStack
+
+import concourse.mybir as mybir
+from concourse.masks import make_identity
+
+BF16 = mybir.dt.bfloat16
+F32 = mybir.dt.float32
+U32 = mybir.dt.uint32
+U8 = mybir.dt.uint8
+FP8X4 = mybir.dt.float8_e4m3fn_x4
+RELU = mybir.ActivationFunctionType.Relu
+MULT = mybir.AluOpType.mult
+ADD = mybir.AluOpType.add
+
+TREES, BATCH, D_H, D_K, D_OUT = 8, 256, 1024, 1024, 256
+FLOPS = 2 * TREES * BATCH * (D_H * D_K + D_K * D_OUT)
+
+P = 128
+PACK = 4
+K_PASS = P * PACK
+PASSES = D_H // K_PASS
+B_TILES = BATCH // P
+CHUNKS = K_PASS // P
+
+UNIT_COLS = K_PASS
+HALVES = D_K // UNIT_COLS
+UNITS_PER_TREE = PASSES * HALVES
+UNITS = TREES * UNITS_PER_TREE
+
+SCALAR_GROUPS = 68
+
+RUN = 4
+RAW_TREES = 4
+
+
+def regroup(copy, grouped, rows):
+    copy(
+        out=grouped.rearrange("p (c i j) -> p c j i", i=RUN, j=PACK),
+        in_=rows.rearrange("p j (c i) -> p c j i", i=RUN),
+    )
+
+
+def tile_randomforestmlp_pa_kernel(tc, h1, W2, b2, W3, b3, out):
+    nc = tc.nc
+    with ExitStack() as ctx:
+        const = ctx.enter_context(tc.tile_pool(name="const", bufs=1))
+        raw = ctx.enter_context(tc.tile_pool(name="raw", bufs=RAW_TREES))
+        w2_stage = ctx.enter_context(tc.tile_pool(name="w2_stage", bufs=4))
+        w2_mx = ctx.enter_context(tc.tile_pool(name="w2_mx", bufs=6))
+        per_tree = ctx.enter_context(tc.tile_pool(name="per_tree", bufs=2))
+        per_half = ctx.enter_context(tc.tile_pool(name="per_half", bufs=3))
+        acc_psum = ctx.enter_context(tc.psum_pool(name="acc_psum", bufs=1))
+        tr_psum = ctx.enter_context(tc.psum_pool(name="tr_psum", bufs=2))
+        h2_psum = ctx.enter_context(tc.psum_pool(name="h2_psum", bufs=4))
+        ctx.enter_context(tc.manual_schedule())
+
+        h1_raw, w2_raw, w3_raw = {}, {}, {}
+        h1_banks, h1_grouped, h1_mx = {}, {}, {}
+        w2_grouped, w2_units = {}, {}
+        w3_grouped, w3_mx = {}, {}
+        h2_banks, h2_plain, h2_grouped, h2_mx = {}, {}, {}, {}
+
+        def live(t):
+            return 0 <= t < TREES
+
+        def load_h1(t):
+            if not live(t):
+                return
+            h1_raw[t] = raw.tile([P, B_TILES * D_H], BF16, name="h1_raw")
+            nc.sync.dma_start(
+                out=h1_raw[t][:], in_=h1[t].rearrange("(p r) k -> p (r k)", r=B_TILES)
+            )
+
+        def load_w2(t, g):
+            if not live(t):
+                return
+            w2_raw[t, g] = raw.tile([P, PACK * D_K], BF16, name="w2_raw%d" % g)
+            rows = W2[t, g * K_PASS : (g + 1) * K_PASS, :]
+            nc.sync.dma_start(
+                out=w2_raw[t, g][:], in_=rows.rearrange("(p j) n -> p (j n)", j=PACK)
+            )
+
+        def load_w3(t):
+            if not live(t):
+                return
+            w3_raw[t] = raw.tile([P, PASSES * PACK * D_OUT], BF16, name="w3_raw")
+            nc.sync.dma_start(
+                out=w3_raw[t][:].rearrange("p (g x) -> p g x", g=PASSES),
+                in_=W3[t].rearrange("(g p j) n -> p g (j n)", p=P, j=PACK),
+            )
+
+        def transpose_h1(t):
+            if not live(t):
+                return
+            words = h1_raw[t][:].bitcast(F32).rearrange(
+                "p (r g w u) -> p r g u w", r=B_TILES, g=PASSES, u=2
+            )
+            for g in range(PASSES):
+                h1_banks[t, g] = tr_psum.tile([P, 2, BATCH], F32, name="h1_bank", tag="tr")
+                for u in range(2):
+                    for r in range(B_TILES):
+                        nc.tensor.transpose(
+                            h1_banks[t, g][:, u, r * P : (r + 1) * P],
+                            words[:, r, g, u, :],
+                            identity[:],
+                        )
+            load_h1(t + RAW_TREES)
+
+        def exit_h1(t, g):
+            if not live(t):
+                return
+            if g == 0:
+                h1_grouped[t] = per_tree.tile(
+                    [P, PASSES * PACK * BATCH], BF16, name="h1_grouped", align_bytes=64
+                )
+            one_pass = h1_grouped[t][:, g * PACK * BATCH : (g + 1) * PACK * BATCH]
+            nc.scalar.copy(
+                out=one_pass.bitcast(F32).rearrange("p (b u) -> p b u", u=2),
+                in_=h1_banks[t, g][:].rearrange("p u b -> p b u"),
+            )
+
+        def quantise(pool, name, grouped, width):
+            codes = pool.tile([P, width], U32, name=name + "_codes", align_bytes=64)
+            scales = pool.tile([P, width], U8, name=name + "_scales", align_bytes=64)
+            nc.vector.quantize_mx(out=codes[:].bitcast(FP8X4), scales=scales[:], in_=grouped[:])
+            return codes, scales
+
+        def quantise_h1(t):
+            if live(t):
+                h1_mx[t] = quantise(per_tree, "h1", h1_grouped[t], PASSES * BATCH)
+
+        def regroup_w2(unit):
+            if not 0 <= unit < UNITS:
+                return
+            t, rest = divmod(unit, UNITS_PER_TREE)
+            g, half = divmod(rest, HALVES)
+            w2_grouped[unit] = w2_stage.tile(
+                [P, PACK * UNIT_COLS], BF16, name="w2_grouped", align_bytes=64
+            )
+            rows = w2_raw[t, g][:].rearrange("p (j n) -> p j n", j=PACK)
+            rows = rows[:, :, half * UNIT_COLS : (half + 1) * UNIT_COLS]
+            source = rows.rearrange("p j (m i) -> p m j i", i=PACK)
+            target = w2_grouped[unit][:].rearrange("p (i m j) -> p m j i", i=PACK, j=PACK)
+            nc.scalar.copy(out=target[:, :SCALAR_GROUPS], in_=source[:, :SCALAR_GROUPS])
+            nc.vector.tensor_copy(out=target[:, SCALAR_GROUPS:], in_=source[:, SCALAR_GROUPS:])
+            if half == HALVES - 1:
+                load_w2(t + RAW_TREES, g)
+
+        def quantise_w2(unit):
+            if 0 <= unit < UNITS:
+                w2_units[unit] = quantise(w2_mx, "w2", w2_grouped[unit], UNIT_COLS)
+
+        def w2_slot(unit):
+            regroup_w2(unit + 1)
+            quantise_w2(unit)
+
+        def regroup_w3(t, g):
+            if not live(t):
+                return
+            if g == 0:
+                w3_grouped[t] = per_tree.tile(
+                    [P, PASSES * PACK * D_OUT], BF16, name="w3_grouped", align_bytes=64
+                )
+            cols = slice(g * PACK * D_OUT, (g + 1) * PACK * D_OUT)
+            regroup(
+                nc.vector.tensor_copy,
+                w3_grouped[t][:, cols],
+                w3_raw[t][:, cols].rearrange("p (j n) -> p j n", j=PACK),
+            )
+            if g == PASSES - 1:
+                load_w3(t + RAW_TREES)
+
+        def quantise_w3(t):
+            if live(t):
+                w3_mx[t] = quantise(per_tree, "w3", w3_grouped[t], PASSES * D_OUT)
+
+        def stage1(t, half):
+            if not live(t):
+                return
+            h1_codes, h1_scales = h1_mx[t]
+            for c in range(CHUNKS):
+                if c % 2 == 0:
+                    bank = h2_psum.tile([P, 2, BATCH], F32, name="h2_bank")
+                    h2_banks[t, half, c // 2] = bank
+                m_cols = slice(c * P, (c + 1) * P)
+                for g in range(PASSES):
+                    w2_codes, w2_scales = w2_units[(t * PASSES + g) * HALVES + half]
+                    b_cols = slice(g * BATCH, (g + 1) * BATCH)
+                    nc.tensor.matmul_mx(
+                        out=bank[:, c % 2, :],
+                        lhsT=w2_codes[:, m_cols].bitcast(FP8X4),
+                        lhsT_scale=w2_scales[:, m_cols],
+                        rhs=h1_codes[:, b_cols].bitcast(FP8X4),
+                        rhs_scale=h1_scales[:, b_cols],
+                        start=(g == 0),
+                        stop=(g == PASSES - 1),
+                    )
+
+        def exit_h2(t, half):
+            if not live(t):
+                return
+            h2_plain[t, half] = per_half.tile([P, CHUNKS * BATCH], BF16, name="h2_plain")
+            for c in range(CHUNKS):
+                column = c * TREES * HALVES + t * HALVES + half
+                nc.scalar.activation(
+                    out=h2_plain[t, half][:, c * BATCH : (c + 1) * BATCH],
+                    in_=h2_banks[t, half, c // 2][:, c % 2, :],
+                    func=RELU,
+                    bias=b2_columns[:, column : column + 1],
+                    scale=1.0,
+                )
+
+        def regroup_h2(t, half):
+            if not live(t):
+                return
+            h2_grouped[t, half] = per_half.tile(
+                [P, PACK * BATCH], BF16, name="h2_grouped", align_bytes=64
+            )
+            regroup(
+                nc.vector.tensor_copy,
+                h2_grouped[t, half][:],
+                h2_plain[t, half][:].rearrange("p (j b) -> p j b", j=PACK),
+            )
+
+        def quantise_h2(t, half):
+            if live(t):
+                h2_mx[t, half] = quantise(per_half, "h2", h2_grouped[t, half], BATCH)
+
+        def stage2(t, g):
+            if not live(t):
+                return
+            h2_codes, h2_scales = h2_mx[t, g]
+            w3_codes, w3_scales = w3_mx[t]
+            n_cols = slice(g * D_OUT, (g + 1) * D_OUT)
+            for r in range(B_TILES):
+                m_cols = slice(r * P, (r + 1) * P)
+                nc.tensor.matmul_mx(
+                    out=acc[r][:],
+                    lhsT=h2_codes[:, m_cols].bitcast(FP8X4),
+                    lhsT_scale=h2_scales[:, m_cols],
+                    rhs=w3_codes[:, n_cols].bitcast(FP8X4),
+                    rhs_scale=w3_scales[:, n_cols],
+                    start=(t == 0 and g == 0),
+                    stop=(t == TREES - 1 and g == PASSES - 1),
+                )
+
+        b2_rows = const.tile([P, UNIT_COLS], BF16, name="b2_rows")
+        b3_rows = const.tile([P, D_OUT], BF16, name="b3_rows")
+        ones = const.tile([P, P], BF16, name="ones")
+        nc.vector.memset(b2_rows[:], 0.0)
+        nc.vector.memset(b3_rows[:], 0.0)
+        nc.vector.memset(ones[:], 1.0)
+        nc.scalar.dma_start(
+            out=b2_rows[: TREES * HALVES, :], in_=b2.rearrange("t (h n) -> (t h) n", h=HALVES)
+        )
+        nc.scalar.dma_start(out=b3_rows[:TREES, :], in_=b3)
+        for t in range(RAW_TREES):
+            load_h1(t)
+            for g in range(PASSES):
+                load_w2(t, g)
+            load_w3(t)
+        identity = const.tile([P, P], F32, name="identity")
+        make_identity(nc, identity[:])
+        acc = [acc_psum.tile([P, D_OUT], F32, name="acc%d" % r) for r in range(B_TILES)]
+
+        transpose_h1(0)
+        exit_h1(0, 0)
+        exit_h1(0, 1)
+
+        b2_rows_f32 = const.tile([P, UNIT_COLS], F32, name="b2_rows_f32")
+        nc.vector.tensor_copy(
+            out=b2_rows_f32[:].rearrange("p (j m) -> p m j", j=PACK),
+            in_=b2_rows[:].rearrange("p (m j) -> p m j", j=PACK),
+        )
+        b2_bank = tr_psum.tile([P, PACK, P], F32, name="b2_bank", tag="tr")
+        for j in range(PACK):
+            nc.tensor.transpose(b2_bank[:, j, :], b2_rows_f32[:, j * P : (j + 1) * P], identity[:])
+        b2_columns = const.tile([P, PACK * TREES * HALVES], F32, name="b2_columns")
+        nc.vector.tensor_copy(
+            out=b2_columns[:].rearrange("p (j r) -> p j r", j=PACK),
+            in_=b2_bank[:, :, : TREES * HALVES],
+        )
+        b3_bank = tr_psum.tile([P, 2, BATCH], F32, name="b3_bank", tag="tr")
+        nc.tensor.matmul(out=b3_bank[:, 0, :], lhsT=ones[:], rhs=b3_rows[:], start=True, stop=True)
+        b3_mean = const.tile([P, D_OUT], F32, name="b3_mean")
+        nc.scalar.mul(out=b3_mean[:], in_=b3_bank[:, 0, :], mul=1.0 / TREES)
+
+        quantise_h1(0)
+        regroup_w2(0)
+
+        for t in range(TREES + 1):
+            first = t * UNITS_PER_TREE
+            w2_slot(first)
+            exit_h2(t - 1, 1)
+            regroup_h2(t - 1, 0)
+            regroup_w3(t, 0)
+
+            w2_slot(first + 1)
+            transpose_h1(t + 1)
+            exit_h1(t + 1, 0)
+            quantise_h2(t - 1, 0)
+            stage2(t - 1, 0)
+            regroup_h2(t - 1, 1)
+
+            w2_slot(first + 2)
+            stage1(t, 0)
+            exit_h1(t + 1, 1)
+            quantise_h2(t - 1, 1)
+            stage2(t - 1, 1)
+            regroup_w3(t, 1)
+
+            w2_slot(first + 3)
+            stage1(t, 1)
+            exit_h2(t, 0)
+            quantise_w3(t)
+            quantise_h1(t + 1)
+
+        out_rows = const.tile([P, B_TILES, D_OUT], F32, name="out_rows")
+        for r in range(B_TILES):
+            nc.vector.scalar_tensor_tensor(
+                out=out_rows[:, r, :],
+                in0=acc[r][:],
+                scalar=1.0 / TREES,
+                in1=b3_mean[:],
+                op0=MULT,
+                op1=ADD,
+            )
+        nc.sync.dma_start(out=out.rearrange("(p r) n -> p r n", r=B_TILES), in_=out_rows[:])

@@ -11,6 +11,7 @@ FP8X4 = mybir.dt.float8_e4m3fn_x4
 RELU = mybir.ActivationFunctionType.Relu
 MULT = mybir.AluOpType.mult
 ADD = mybir.AluOpType.add
+MAX = mybir.AluOpType.max
 
 TREES, BATCH, D_H, D_K, D_OUT = 8, 256, 1024, 1024, 256
 FLOPS = 2 * TREES * BATCH * (D_H * D_K + D_K * D_OUT)
@@ -71,14 +72,16 @@ def tile_randomforestmlp_pa_kernel(tc, h1, W2, b2, W3, b3, out):
                 out=h1_raw[t][:], in_=h1[t].rearrange("(p r) k -> p (r k)", r=B_TILES)
             )
 
-        def load_w2(t, g):
+        def load_w2(t, g, pieces=1):
             if not live(t):
                 return
             w2_raw[t, g] = raw.tile([P, PACK * D_K], BF16, name="w2_raw%d" % g)
-            rows = W2[t, g * K_PASS : (g + 1) * K_PASS, :]
-            nc.sync.dma_start(
-                out=w2_raw[t, g][:], in_=rows.rearrange("(p j) n -> p (j n)", j=PACK)
-            )
+            rows = W2[t, g * K_PASS : (g + 1) * K_PASS, :].rearrange("(p j) n -> p j n", j=PACK)
+            tile_rows = w2_raw[t, g][:].rearrange("p (j n) -> p j n", j=PACK)
+            width = D_K // pieces
+            for piece in range(pieces):
+                cols = slice(piece * width, (piece + 1) * width)
+                nc.sync.dma_start(out=tile_rows[:, :, cols], in_=rows[:, :, cols])
 
         def load_w3(t):
             if not live(t):
@@ -200,15 +203,18 @@ def tile_randomforestmlp_pa_kernel(tc, h1, W2, b2, W3, b3, out):
             if not live(t):
                 return
             h2_plain[t, half] = per_half.tile([P, CHUNKS * BATCH], BF16, name="h2_plain")
+            last = t == TREES - 1 and half == HALVES - 1
             for c in range(CHUNKS):
                 column = c * TREES * HALVES + t * HALVES + half
-                nc.scalar.activation(
-                    out=h2_plain[t, half][:, c * BATCH : (c + 1) * BATCH],
-                    in_=h2_banks[t, half, c // 2][:, c % 2, :],
-                    func=RELU,
-                    bias=b2_columns[:, column : column + 1],
-                    scale=1.0,
-                )
+                bias = b2_columns[:, column : column + 1]
+                sums = h2_banks[t, half, c // 2][:, c % 2, :]
+                rows = h2_plain[t, half][:, c * BATCH : (c + 1) * BATCH]
+                if last and c >= CHUNKS // 2:
+                    nc.vector.tensor_scalar(
+                        out=rows, in0=sums, scalar1=bias, scalar2=0.0, op0=ADD, op1=MAX
+                    )
+                else:
+                    nc.scalar.activation(out=rows, in_=sums, func=RELU, bias=bias, scale=1.0)
 
         def regroup_h2(t, half):
             if not live(t):
@@ -254,48 +260,57 @@ def tile_randomforestmlp_pa_kernel(tc, h1, W2, b2, W3, b3, out):
             out=b2_rows[: TREES * HALVES, :], in_=b2.rearrange("t (h n) -> (t h) n", h=HALVES)
         )
         nc.scalar.dma_start(out=b3_rows[:TREES, :], in_=b3)
+        warm = const.tile([P, 1], F32, name="warm")
+        nc.scalar.activation(out=warm[:], in_=ones[:, :1], func=RELU)
         for t in range(RAW_TREES):
+            load_w2(t, 0, pieces=HALVES if t == 0 else 1)
             load_h1(t)
-            for g in range(PASSES):
-                load_w2(t, g)
+            load_w2(t, 1)
             load_w3(t)
         identity = const.tile([P, P], F32, name="identity")
         make_identity(nc, identity[:])
         acc = [acc_psum.tile([P, D_OUT], F32, name="acc%d" % r) for r in range(B_TILES)]
 
-        transpose_h1(0)
-        exit_h1(0, 0)
-        exit_h1(0, 1)
-
-        b2_rows_f32 = const.tile([P, UNIT_COLS], F32, name="b2_rows_f32")
-        nc.vector.tensor_copy(
-            out=b2_rows_f32[:].rearrange("p (j m) -> p m j", j=PACK),
-            in_=b2_rows[:].rearrange("p (m j) -> p m j", j=PACK),
-        )
-        b2_bank = tr_psum.tile([P, PACK, P], F32, name="b2_bank", tag="tr")
-        for j in range(PACK):
-            nc.tensor.transpose(b2_bank[:, j, :], b2_rows_f32[:, j * P : (j + 1) * P], identity[:])
         b2_columns = const.tile([P, PACK * TREES * HALVES], F32, name="b2_columns")
-        nc.vector.tensor_copy(
-            out=b2_columns[:].rearrange("p (j r) -> p j r", j=PACK),
-            in_=b2_bank[:, :, : TREES * HALVES],
-        )
-        b3_bank = tr_psum.tile([P, 2, BATCH], F32, name="b3_bank", tag="tr")
-        nc.tensor.matmul(out=b3_bank[:, 0, :], lhsT=ones[:], rhs=b3_rows[:], start=True, stop=True)
         b3_mean = const.tile([P, D_OUT], F32, name="b3_mean")
-        nc.scalar.mul(out=b3_mean[:], in_=b3_bank[:, 0, :], mul=1.0 / TREES)
 
-        quantise_h1(0)
+        def prepare_b2():
+            b2_rows_f32 = const.tile([P, UNIT_COLS], F32, name="b2_rows_f32")
+            nc.vector.tensor_copy(
+                out=b2_rows_f32[:].rearrange("p (j m) -> p m j", j=PACK),
+                in_=b2_rows[:].rearrange("p (m j) -> p m j", j=PACK),
+            )
+            b2_bank = tr_psum.tile([P, PACK, P], F32, name="b2_bank", tag="tr")
+            for j in range(PACK):
+                nc.tensor.transpose(b2_bank[:, j, :], b2_rows_f32[:, j * P : (j + 1) * P], identity[:])
+            nc.vector.tensor_copy(
+                out=b2_columns[:].rearrange("p (j r) -> p j r", j=PACK),
+                in_=b2_bank[:, :, : TREES * HALVES],
+            )
+
+        def prepare_b3():
+            b3_bank = tr_psum.tile([P, 2, BATCH], F32, name="b3_bank", tag="tr")
+            nc.tensor.matmul(out=b3_bank[:, 0, :], lhsT=ones[:], rhs=b3_rows[:], start=True, stop=True)
+            nc.scalar.mul(out=b3_mean[:], in_=b3_bank[:, 0, :], mul=1.0 / TREES)
+
         regroup_w2(0)
+        transpose_h1(0)
 
         for t in range(TREES + 1):
             first = t * UNITS_PER_TREE
             w2_slot(first)
-            exit_h2(t - 1, 1)
+            if t == 0:
+                exit_h1(0, 0)
+                exit_h1(0, 1)
             regroup_h2(t - 1, 0)
-            regroup_w3(t, 0)
+            exit_h2(t - 1, 1)
+            quantise_w3(t - 1)
 
             w2_slot(first + 1)
+            if t == 0:
+                quantise_h1(0)
+            if t == 1:
+                prepare_b3()
             transpose_h1(t + 1)
             exit_h1(t + 1, 0)
             quantise_h2(t - 1, 0)
@@ -303,16 +318,18 @@ def tile_randomforestmlp_pa_kernel(tc, h1, W2, b2, W3, b3, out):
             regroup_h2(t - 1, 1)
 
             w2_slot(first + 2)
+            if t == 0:
+                prepare_b2()
             stage1(t, 0)
             exit_h1(t + 1, 1)
             quantise_h2(t - 1, 1)
             stage2(t - 1, 1)
-            regroup_w3(t, 1)
+            regroup_w3(t, 0)
 
             w2_slot(first + 3)
             stage1(t, 1)
             exit_h2(t, 0)
-            quantise_w3(t)
+            regroup_w3(t, 1)
             quantise_h1(t + 1)
 
         out_rows = const.tile([P, B_TILES, D_OUT], F32, name="out_rows")

@@ -28,7 +28,9 @@ HALVES = D_K // UNIT_COLS
 UNITS_PER_TREE = PASSES * HALVES
 UNITS = TREES * UNITS_PER_TREE
 
-SCALAR_GROUPS = 68
+SCALAR_GROUPS = 48
+TENSOR_GROUPS = 32
+FIRST_SCALAR_GROUPS = 72
 
 RUN = 4
 RAW_TREES = 4
@@ -46,18 +48,19 @@ def tile_randomforestmlp_pa_kernel(tc, h1, W2, b2, W3, b3, out):
     with ExitStack() as ctx:
         const = ctx.enter_context(tc.tile_pool(name="const", bufs=1))
         raw = ctx.enter_context(tc.tile_pool(name="raw", bufs=RAW_TREES))
-        w2_stage = ctx.enter_context(tc.tile_pool(name="w2_stage", bufs=4))
+        w2_stage = ctx.enter_context(tc.tile_pool(name="w2_stage", bufs=5))
         w2_mx = ctx.enter_context(tc.tile_pool(name="w2_mx", bufs=6))
         per_tree = ctx.enter_context(tc.tile_pool(name="per_tree", bufs=2))
         per_half = ctx.enter_context(tc.tile_pool(name="per_half", bufs=3))
         acc_psum = ctx.enter_context(tc.psum_pool(name="acc_psum", bufs=1))
         tr_psum = ctx.enter_context(tc.psum_pool(name="tr_psum", bufs=2))
-        h2_psum = ctx.enter_context(tc.psum_pool(name="h2_psum", bufs=4))
+        mv_psum = ctx.enter_context(tc.psum_pool(name="mv_psum", bufs=1))
+        h2_psum = ctx.enter_context(tc.psum_pool(name="h2_psum", bufs=3))
         ctx.enter_context(tc.manual_schedule())
 
         h1_raw, w2_raw, w3_raw = {}, {}, {}
         h1_banks, h1_grouped, h1_mx = {}, {}, {}
-        w2_grouped, w2_units = {}, {}
+        w2_banks, w2_grouped, w2_units = {}, {}, {}
         w3_grouped, w3_mx = {}, {}
         h2_banks, h2_plain, h2_grouped, h2_mx = {}, {}, {}, {}
 
@@ -72,25 +75,27 @@ def tile_randomforestmlp_pa_kernel(tc, h1, W2, b2, W3, b3, out):
                 out=h1_raw[t][:], in_=h1[t].rearrange("(p r) k -> p (r k)", r=B_TILES)
             )
 
-        def load_w2(t, g, pieces=1):
+        def load_w2(t, g, half=None):
             if not live(t):
                 return
-            w2_raw[t, g] = raw.tile([P, PACK * D_K], BF16, name="w2_raw%d" % g)
-            rows = W2[t, g * K_PASS : (g + 1) * K_PASS, :].rearrange("(p j) n -> p j n", j=PACK)
-            tile_rows = w2_raw[t, g][:].rearrange("p (j n) -> p j n", j=PACK)
-            width = D_K // pieces
-            for piece in range(pieces):
-                cols = slice(piece * width, (piece + 1) * width)
-                nc.sync.dma_start(out=tile_rows[:, :, cols], in_=rows[:, :, cols])
+            if (t, g) not in w2_raw:
+                w2_raw[t, g] = raw.tile([P, PACK * D_K], BF16, name="w2_raw%d" % g)
+            cols = slice(0, D_K) if half is None else slice(half * UNIT_COLS, (half + 1) * UNIT_COLS)
+            nc.sync.dma_start(
+                out=w2_raw[t, g][:].rearrange("p (j n) -> p j n", j=PACK)[:, :, cols],
+                in_=W2[t, g * K_PASS : (g + 1) * K_PASS, :].rearrange("(p j) n -> p j n", j=PACK)[:, :, cols],
+            )
 
-        def load_w3(t):
+        def load_w3(t, pieces=1):
             if not live(t):
                 return
             w3_raw[t] = raw.tile([P, PASSES * PACK * D_OUT], BF16, name="w3_raw")
-            nc.sync.dma_start(
-                out=w3_raw[t][:].rearrange("p (g x) -> p g x", g=PASSES),
-                in_=W3[t].rearrange("(g p j) n -> p g (j n)", p=P, j=PACK),
-            )
+            tile_rows = w3_raw[t][:].rearrange("p (g x) -> p g x", g=PASSES)
+            rows = W3[t].rearrange("(g p j) n -> p g (j n)", p=P, j=PACK)
+            count = PASSES // pieces
+            for piece in range(pieces):
+                some = slice(piece * count, (piece + 1) * count)
+                nc.sync.dma_start(out=tile_rows[:, some], in_=rows[:, some])
 
         def transpose_h1(t):
             if not live(t):
@@ -132,30 +137,66 @@ def tile_randomforestmlp_pa_kernel(tc, h1, W2, b2, W3, b3, out):
             if live(t):
                 h1_mx[t] = quantise(per_tree, "h1", h1_grouped[t], PASSES * BATCH)
 
-        def regroup_w2(unit):
-            if not 0 <= unit < UNITS:
-                return
+        def w2_rows(unit):
             t, rest = divmod(unit, UNITS_PER_TREE)
             g, half = divmod(rest, HALVES)
-            w2_grouped[unit] = w2_stage.tile(
-                [P, PACK * UNIT_COLS], BF16, name="w2_grouped", align_bytes=64
-            )
             rows = w2_raw[t, g][:].rearrange("p (j n) -> p j n", j=PACK)
-            rows = rows[:, :, half * UNIT_COLS : (half + 1) * UNIT_COLS]
-            source = rows.rearrange("p j (m i) -> p m j i", i=PACK)
+            return rows[:, :, half * UNIT_COLS : (half + 1) * UNIT_COLS]
+
+        def move_w2(unit):
+            if not 1 <= unit < UNITS:
+                return
+            cols = slice(PACK * SCALAR_GROUPS, PACK * (SCALAR_GROUPS + TENSOR_GROUPS))
+            w2_banks[unit] = mv_psum.tile([P, PACK, TENSOR_GROUPS, PACK], BF16, name="w2_bank")
+            nc.tensor.matmul(
+                out=w2_banks[unit][:].rearrange("p i m j -> p j m i"),
+                lhsT=identity_bf16[:],
+                rhs=w2_rows(unit)[:, :, cols].rearrange("p j (m i) -> p j m i", i=PACK),
+                start=True,
+                stop=True,
+            )
+
+        def w2_views(unit):
+            if unit not in w2_grouped:
+                w2_grouped[unit] = w2_stage.tile(
+                    [P, PACK * UNIT_COLS], BF16, name="w2_grouped", align_bytes=64
+                )
+            source = w2_rows(unit).rearrange("p j (m i) -> p m j i", i=PACK)
             target = w2_grouped[unit][:].rearrange("p (i m j) -> p m j i", i=PACK, j=PACK)
-            nc.scalar.copy(out=target[:, :SCALAR_GROUPS], in_=source[:, :SCALAR_GROUPS])
-            nc.vector.tensor_copy(out=target[:, SCALAR_GROUPS:], in_=source[:, SCALAR_GROUPS:])
+            return source, target
+
+        def regroup_w2_scalar(unit):
+            if not 0 <= unit < UNITS:
+                return
+            source, target = w2_views(unit)
+            first = SCALAR_GROUPS if unit >= 1 else FIRST_SCALAR_GROUPS
+            nc.scalar.copy(out=target[:, :first], in_=source[:, :first])
+
+        def exit_w2(unit):
+            if unit not in w2_banks:
+                return
+            first, last = SCALAR_GROUPS, SCALAR_GROUPS + TENSOR_GROUPS
+            nc.scalar.copy(
+                out=w2_grouped[unit][:].rearrange("p (i x) -> p i x", i=PACK)[
+                    :, :, PACK * first : PACK * last
+                ],
+                in_=w2_banks[unit][:].rearrange("p i m j -> p i (m j)"),
+            )
+
+        def regroup_w2_vector(unit):
+            if not 0 <= unit < UNITS:
+                return
+            source, target = w2_views(unit)
+            last = SCALAR_GROUPS + TENSOR_GROUPS if unit >= 1 else FIRST_SCALAR_GROUPS
+            nc.vector.tensor_copy(out=target[:, last:], in_=source[:, last:])
+            t, rest = divmod(unit, UNITS_PER_TREE)
+            g, half = divmod(rest, HALVES)
             if half == HALVES - 1:
                 load_w2(t + RAW_TREES, g)
 
         def quantise_w2(unit):
             if 0 <= unit < UNITS:
                 w2_units[unit] = quantise(w2_mx, "w2", w2_grouped[unit], UNIT_COLS)
-
-        def w2_slot(unit):
-            regroup_w2(unit + 1)
-            quantise_w2(unit)
 
         def regroup_w3(t, g):
             if not live(t):
@@ -262,75 +303,115 @@ def tile_randomforestmlp_pa_kernel(tc, h1, W2, b2, W3, b3, out):
         nc.scalar.dma_start(out=b3_rows[:TREES, :], in_=b3)
         warm = const.tile([P, 1], F32, name="warm")
         nc.scalar.activation(out=warm[:], in_=ones[:, :1], func=RELU)
-        for t in range(RAW_TREES):
-            load_w2(t, 0, pieces=HALVES if t == 0 else 1)
+        load_w2(0, 0, 0)
+        load_w2(0, 0, 1)
+        load_h1(0)
+        load_w3(0, pieces=PASSES)
+        load_w2(0, 1, 0)
+        load_w2(0, 1, 1)
+        load_w2(1, 0, 0)
+        load_h1(1)
+        load_w2(1, 0, 1)
+        load_w2(1, 1)
+        load_w3(1)
+        for t in range(2, RAW_TREES):
             load_h1(t)
-            load_w2(t, 1)
+            for g in range(PASSES):
+                load_w2(t, g)
             load_w3(t)
         identity = const.tile([P, P], F32, name="identity")
         make_identity(nc, identity[:])
+        identity_bf16 = const.tile([P, P], BF16, name="identity_bf16")
+        make_identity(nc, identity_bf16[:])
         acc = [acc_psum.tile([P, D_OUT], F32, name="acc%d" % r) for r in range(B_TILES)]
 
         b2_columns = const.tile([P, PACK * TREES * HALVES], F32, name="b2_columns")
         b3_mean = const.tile([P, D_OUT], F32, name="b3_mean")
 
-        def prepare_b2():
+        b2_banks = []
+
+        def prepare_b2_rows():
             b2_rows_f32 = const.tile([P, UNIT_COLS], F32, name="b2_rows_f32")
             nc.vector.tensor_copy(
                 out=b2_rows_f32[:].rearrange("p (j m) -> p m j", j=PACK),
                 in_=b2_rows[:].rearrange("p (m j) -> p m j", j=PACK),
             )
-            b2_bank = tr_psum.tile([P, PACK, P], F32, name="b2_bank", tag="tr")
+            b2_bank = h2_psum.tile([P, PACK, P], F32, name="b2_bank", tag="h2_bank")
             for j in range(PACK):
                 nc.tensor.transpose(b2_bank[:, j, :], b2_rows_f32[:, j * P : (j + 1) * P], identity[:])
+            b2_banks.append(b2_bank)
+
+        def prepare_b2_columns():
             nc.vector.tensor_copy(
                 out=b2_columns[:].rearrange("p (j r) -> p j r", j=PACK),
-                in_=b2_bank[:, :, : TREES * HALVES],
+                in_=b2_banks[0][:, :, : TREES * HALVES],
             )
 
         def prepare_b3():
-            b3_bank = tr_psum.tile([P, 2, BATCH], F32, name="b3_bank", tag="tr")
+            b3_bank = h2_psum.tile([P, 2, BATCH], F32, name="b3_bank", tag="h2_bank")
             nc.tensor.matmul(out=b3_bank[:, 0, :], lhsT=ones[:], rhs=b3_rows[:], start=True, stop=True)
             nc.scalar.mul(out=b3_mean[:], in_=b3_bank[:, 0, :], mul=1.0 / TREES)
 
-        regroup_w2(0)
+        regroup_w2_scalar(0)
+        regroup_w2_vector(0)
+        move_w2(1)
         transpose_h1(0)
+        regroup_w2_scalar(1)
+        exit_h1(0, 0)
+        exit_h1(0, 1)
 
         for t in range(TREES + 1):
             first = t * UNITS_PER_TREE
-            w2_slot(first)
+            exit_w2(first + 1)
+            move_w2(first + 2)
+            regroup_w2_scalar(first + 2)
+            regroup_w2_vector(first + 1)
+            quantise_w2(first)
             if t == 0:
-                exit_h1(0, 0)
-                exit_h1(0, 1)
+                regroup_w3(0, 0)
+                regroup_w3(0, 1)
+                prepare_b2_rows()
             regroup_h2(t - 1, 0)
             exit_h2(t - 1, 1)
             quantise_w3(t - 1)
 
-            w2_slot(first + 1)
+            exit_w2(first + 2)
+            move_w2(first + 3)
+            regroup_w2_scalar(first + 3)
+            regroup_w2_vector(first + 2)
+            quantise_w2(first + 1)
+            quantise_h1(t)
             if t == 0:
-                quantise_h1(0)
+                prepare_b2_columns()
             if t == 1:
                 prepare_b3()
-            transpose_h1(t + 1)
-            exit_h1(t + 1, 0)
             quantise_h2(t - 1, 0)
             stage2(t - 1, 0)
             regroup_h2(t - 1, 1)
 
-            w2_slot(first + 2)
-            if t == 0:
-                prepare_b2()
+            exit_w2(first + 3)
+            move_w2(first + 4)
+            regroup_w2_scalar(first + 4)
+            regroup_w2_vector(first + 3)
+            quantise_w2(first + 2)
+            transpose_h1(t + 1)
+            exit_h1(t + 1, 0)
             stage1(t, 0)
-            exit_h1(t + 1, 1)
             quantise_h2(t - 1, 1)
             stage2(t - 1, 1)
-            regroup_w3(t, 0)
+            if t > 0:
+                regroup_w3(t, 0)
 
-            w2_slot(first + 3)
-            stage1(t, 1)
+            exit_w2(first + 4)
+            move_w2(first + 5)
+            regroup_w2_scalar(first + 5)
             exit_h2(t, 0)
-            regroup_w3(t, 1)
-            quantise_h1(t + 1)
+            exit_h1(t + 1, 1)
+            regroup_w2_vector(first + 4)
+            quantise_w2(first + 3)
+            stage1(t, 1)
+            if t > 0:
+                regroup_w3(t, 1)
 
         out_rows = const.tile([P, B_TILES, D_OUT], F32, name="out_rows")
         for r in range(B_TILES):

@@ -23,24 +23,14 @@ PASSES = D_H // K_PASS
 B_TILES = BATCH // P
 CHUNKS = K_PASS // P
 
-UNIT_COLS = K_PASS
-HALVES = D_K // UNIT_COLS
-UNITS_PER_TREE = PASSES * HALVES
-UNITS = TREES * UNITS_PER_TREE
+HALVES = D_K // K_PASS
+GROUPS = K_PASS // PACK
 
 SCALAR_GROUPS = 48
 TENSOR_GROUPS = 32
 FIRST_SCALAR_GROUPS = 72
-
 RUN = 4
 RAW_TREES = 4
-
-
-def regroup(copy, grouped, rows):
-    copy(
-        out=grouped.rearrange("p (c i j) -> p c j i", i=RUN, j=PACK),
-        in_=rows.rearrange("p j (c i) -> p c j i", i=RUN),
-    )
 
 
 def tile_randomforestmlp_pa_kernel(tc, h1, W2, b2, W3, b3, out):
@@ -48,19 +38,17 @@ def tile_randomforestmlp_pa_kernel(tc, h1, W2, b2, W3, b3, out):
     with ExitStack() as ctx:
         const = ctx.enter_context(tc.tile_pool(name="const", bufs=1))
         raw = ctx.enter_context(tc.tile_pool(name="raw", bufs=RAW_TREES))
-        w2_stage = ctx.enter_context(tc.tile_pool(name="w2_stage", bufs=5))
-        w2_mx = ctx.enter_context(tc.tile_pool(name="w2_mx", bufs=6))
-        per_tree = ctx.enter_context(tc.tile_pool(name="per_tree", bufs=2))
-        per_half = ctx.enter_context(tc.tile_pool(name="per_half", bufs=3))
+        stage = ctx.enter_context(tc.tile_pool(name="stage", bufs=3))
+        mx = ctx.enter_context(tc.tile_pool(name="mx", bufs=4))
         acc_psum = ctx.enter_context(tc.psum_pool(name="acc_psum", bufs=1))
-        tr_psum = ctx.enter_context(tc.psum_pool(name="tr_psum", bufs=2))
+        tr_psum = ctx.enter_context(tc.psum_pool(name="tr_psum", bufs=1))
         mv_psum = ctx.enter_context(tc.psum_pool(name="mv_psum", bufs=1))
-        h2_psum = ctx.enter_context(tc.psum_pool(name="h2_psum", bufs=3))
+        h2_psum = ctx.enter_context(tc.psum_pool(name="h2_psum", bufs=4))
         ctx.enter_context(tc.manual_schedule())
 
         h1_raw, w2_raw, w3_raw = {}, {}, {}
         h1_banks, h1_grouped, h1_mx = {}, {}, {}
-        w2_banks, w2_grouped, w2_units = {}, {}, {}
+        w2_banks, w2_grouped, w2_mx = {}, {}, {}
         w3_grouped, w3_mx = {}, {}
         h2_banks, h2_plain, h2_grouped, h2_mx = {}, {}, {}, {}
 
@@ -80,45 +68,42 @@ def tile_randomforestmlp_pa_kernel(tc, h1, W2, b2, W3, b3, out):
                 return
             if (t, g) not in w2_raw:
                 w2_raw[t, g] = raw.tile([P, PACK * D_K], BF16, name="w2_raw%d" % g)
-            cols = slice(0, D_K) if half is None else slice(half * UNIT_COLS, (half + 1) * UNIT_COLS)
+            cols = slice(0, D_K) if half is None else slice(half * K_PASS, (half + 1) * K_PASS)
+            rows = W2[t, g * K_PASS : (g + 1) * K_PASS, :].rearrange("(p j) n -> p j n", j=PACK)
             nc.sync.dma_start(
                 out=w2_raw[t, g][:].rearrange("p (j n) -> p j n", j=PACK)[:, :, cols],
-                in_=W2[t, g * K_PASS : (g + 1) * K_PASS, :].rearrange("(p j) n -> p j n", j=PACK)[:, :, cols],
+                in_=rows[:, :, cols],
             )
 
-        def load_w3(t, pieces=1):
+        def load_w3(t):
             if not live(t):
                 return
             w3_raw[t] = raw.tile([P, PASSES * PACK * D_OUT], BF16, name="w3_raw")
-            tile_rows = w3_raw[t][:].rearrange("p (g x) -> p g x", g=PASSES)
-            rows = W3[t].rearrange("(g p j) n -> p g (j n)", p=P, j=PACK)
-            count = PASSES // pieces
-            for piece in range(pieces):
-                some = slice(piece * count, (piece + 1) * count)
-                nc.sync.dma_start(out=tile_rows[:, some], in_=rows[:, some])
+            nc.sync.dma_start(
+                out=w3_raw[t][:].rearrange("p (g x) -> p g x", g=PASSES),
+                in_=W3[t].rearrange("(g p j) n -> p g (j n)", p=P, j=PACK),
+            )
 
-        def transpose_h1(t):
+        def transpose_h1(t, g):
             if not live(t):
                 return
             words = h1_raw[t][:].bitcast(F32).rearrange(
                 "p (r g w u) -> p r g u w", r=B_TILES, g=PASSES, u=2
             )
-            for g in range(PASSES):
-                h1_banks[t, g] = tr_psum.tile([P, 2, BATCH], F32, name="h1_bank", tag="tr")
-                for u in range(2):
-                    for r in range(B_TILES):
-                        nc.tensor.transpose(
-                            h1_banks[t, g][:, u, r * P : (r + 1) * P],
-                            words[:, r, g, u, :],
-                            identity[:],
-                        )
-            load_h1(t + RAW_TREES)
+            h1_banks[t, g] = tr_psum.tile([P, 2, BATCH], F32, name="h1_bank")
+            for u in range(2):
+                for r in range(B_TILES):
+                    nc.tensor.transpose(
+                        h1_banks[t, g][:, u, r * P : (r + 1) * P], words[:, r, g, u, :], identity[:]
+                    )
+            if g == PASSES - 1:
+                load_h1(t + RAW_TREES)
 
         def exit_h1(t, g):
             if not live(t):
                 return
             if g == 0:
-                h1_grouped[t] = per_tree.tile(
+                h1_grouped[t] = stage.tile(
                     [P, PASSES * PACK * BATCH], BF16, name="h1_grouped", align_bytes=64
                 )
             one_pass = h1_grouped[t][:, g * PACK * BATCH : (g + 1) * PACK * BATCH]
@@ -127,96 +112,107 @@ def tile_randomforestmlp_pa_kernel(tc, h1, W2, b2, W3, b3, out):
                 in_=h1_banks[t, g][:].rearrange("p u b -> p b u"),
             )
 
-        def quantise(pool, name, grouped, width):
-            codes = pool.tile([P, width], U32, name=name + "_codes", align_bytes=64)
-            scales = pool.tile([P, width], U8, name=name + "_scales", align_bytes=64)
-            nc.vector.quantize_mx(out=codes[:].bitcast(FP8X4), scales=scales[:], in_=grouped[:])
+        def mx_tiles(name, width):
+            codes = mx.tile([P, width], U32, name=name + "_codes", align_bytes=64)
+            scales = mx.tile([P, width], U8, name=name + "_scales", align_bytes=64)
             return codes, scales
+
+        def quantise(tiles, grouped, first, last):
+            codes, scales = tiles
+            nc.vector.quantize_mx(
+                out=codes[:, first:last].bitcast(FP8X4),
+                scales=scales[:, first:last],
+                in_=grouped[:, PACK * first : PACK * last],
+            )
 
         def quantise_h1(t):
             if live(t):
-                h1_mx[t] = quantise(per_tree, "h1", h1_grouped[t], PASSES * BATCH)
+                h1_mx[t] = mx_tiles("h1", PASSES * BATCH)
+                quantise(h1_mx[t], h1_grouped[t], 0, PASSES * BATCH)
 
-        def w2_rows(unit):
-            t, rest = divmod(unit, UNITS_PER_TREE)
-            g, half = divmod(rest, HALVES)
-            rows = w2_raw[t, g][:].rearrange("p (j n) -> p j n", j=PACK)
-            return rows[:, :, half * UNIT_COLS : (half + 1) * UNIT_COLS]
-
-        def move_w2(unit):
-            if not 1 <= unit < UNITS:
-                return
-            cols = slice(PACK * SCALAR_GROUPS, PACK * (SCALAR_GROUPS + TENSOR_GROUPS))
-            w2_banks[unit] = mv_psum.tile([P, PACK, TENSOR_GROUPS, PACK], BF16, name="w2_bank")
-            nc.tensor.matmul(
-                out=w2_banks[unit][:].rearrange("p i m j -> p j m i"),
-                lhsT=identity_bf16[:],
-                rhs=w2_rows(unit)[:, :, cols].rearrange("p j (m i) -> p j m i", i=PACK),
-                start=True,
-                stop=True,
-            )
-
-        def w2_views(unit):
-            if unit not in w2_grouped:
-                w2_grouped[unit] = w2_stage.tile(
-                    [P, PACK * UNIT_COLS], BF16, name="w2_grouped", align_bytes=64
+        def w2_views(t, g):
+            if (t, g) not in w2_grouped:
+                w2_grouped[t, g] = stage.tile(
+                    [P, PACK * D_K], BF16, name="w2_grouped", align_bytes=64
                 )
-            source = w2_rows(unit).rearrange("p j (m i) -> p m j i", i=PACK)
-            target = w2_grouped[unit][:].rearrange("p (i m j) -> p m j i", i=PACK, j=PACK)
+            source = w2_raw[t, g][:].rearrange("p (j h m i) -> p h m j i", j=PACK, h=HALVES, i=PACK)
+            target = w2_grouped[t, g][:].rearrange(
+                "p (h i m j) -> p h m j i", h=HALVES, i=PACK, j=PACK
+            )
             return source, target
 
-        def regroup_w2_scalar(unit):
-            if not 0 <= unit < UNITS:
-                return
-            source, target = w2_views(unit)
-            first = SCALAR_GROUPS if unit >= 1 else FIRST_SCALAR_GROUPS
-            nc.scalar.copy(out=target[:, :first], in_=source[:, :first])
+        def shares(t, g):
+            if (t, g) == (0, 0):
+                return FIRST_SCALAR_GROUPS, FIRST_SCALAR_GROUPS
+            return SCALAR_GROUPS, SCALAR_GROUPS + TENSOR_GROUPS
 
-        def exit_w2(unit):
-            if unit not in w2_banks:
-                return
-            first, last = SCALAR_GROUPS, SCALAR_GROUPS + TENSOR_GROUPS
-            nc.scalar.copy(
-                out=w2_grouped[unit][:].rearrange("p (i x) -> p i x", i=PACK)[
-                    :, :, PACK * first : PACK * last
-                ],
-                in_=w2_banks[unit][:].rearrange("p i m j -> p i (m j)"),
-            )
-
-        def regroup_w2_vector(unit):
-            if not 0 <= unit < UNITS:
-                return
-            source, target = w2_views(unit)
-            last = SCALAR_GROUPS + TENSOR_GROUPS if unit >= 1 else FIRST_SCALAR_GROUPS
-            nc.vector.tensor_copy(out=target[:, last:], in_=source[:, last:])
-            t, rest = divmod(unit, UNITS_PER_TREE)
-            g, half = divmod(rest, HALVES)
-            if half == HALVES - 1:
-                load_w2(t + RAW_TREES, g)
-
-        def quantise_w2(unit):
-            if 0 <= unit < UNITS:
-                w2_units[unit] = quantise(w2_mx, "w2", w2_grouped[unit], UNIT_COLS)
-
-        def regroup_w3(t, g):
+        def regroup_w2_scalar(t, g, first=0, last=HALVES):
             if not live(t):
                 return
-            if g == 0:
-                w3_grouped[t] = per_tree.tile(
-                    [P, PASSES * PACK * D_OUT], BF16, name="w3_grouped", align_bytes=64
+            source, target = w2_views(t, g)
+            stop = shares(t, g)[0]
+            nc.scalar.copy(out=target[:, first:last, :stop], in_=source[:, first:last, :stop])
+
+        def regroup_w2_vector(t, g, first=0, last=HALVES):
+            if not live(t):
+                return
+            source, target = w2_views(t, g)
+            start = shares(t, g)[1]
+            nc.vector.tensor_copy(out=target[:, first:last, start:], in_=source[:, first:last, start:])
+            if last == HALVES:
+                load_w2(t + RAW_TREES, g)
+
+        def move_w2(t, g):
+            start, stop = shares(t, g) if live(t) else (0, 0)
+            if start == stop:
+                return
+            source = w2_views(t, g)[0]
+            w2_banks[t, g] = mv_psum.tile([P, HALVES, PACK, TENSOR_GROUPS, PACK], BF16, name="w2_bank")
+            for half in range(HALVES):
+                nc.tensor.matmul(
+                    out=w2_banks[t, g][:, half].rearrange("p i m j -> p j m i"),
+                    lhsT=identity_bf16[:],
+                    rhs=source[:, half, start:stop].rearrange("p m j i -> p j m i"),
+                    start=True,
+                    stop=True,
                 )
-            cols = slice(g * PACK * D_OUT, (g + 1) * PACK * D_OUT)
-            regroup(
-                nc.vector.tensor_copy,
-                w3_grouped[t][:, cols],
-                w3_raw[t][:, cols].rearrange("p (j n) -> p j n", j=PACK),
+
+        def exit_w2(t, g):
+            if (t, g) not in w2_banks:
+                return
+            start, stop = shares(t, g)
+            blocks = w2_grouped[t, g][:].rearrange("p (b x) -> p b x", b=HALVES * PACK)
+            nc.scalar.copy(
+                out=blocks[:, :, PACK * start : PACK * stop],
+                in_=w2_banks[t, g][:].rearrange("p h i m j -> p (h i) (m j)"),
             )
-            if g == PASSES - 1:
-                load_w3(t + RAW_TREES)
+
+        def quantise_w2(t, g, first=0, last=HALVES):
+            if not live(t):
+                return
+            if first == 0:
+                w2_mx[t, g] = mx_tiles("w2", D_K)
+            quantise(w2_mx[t, g], w2_grouped[t, g], first * K_PASS, last * K_PASS)
+
+        def regroup(grouped, rows):
+            nc.vector.tensor_copy(
+                out=grouped.rearrange("p (h c i j) -> p h c j i", h=grouped.shape[1] // (PACK * BATCH), i=RUN, j=PACK),
+                in_=rows.rearrange("p (h j c i) -> p h c j i", h=grouped.shape[1] // (PACK * BATCH), j=PACK, i=RUN),
+            )
+
+        def regroup_w3(t):
+            if not live(t):
+                return
+            w3_grouped[t] = stage.tile(
+                [P, PASSES * PACK * D_OUT], BF16, name="w3_grouped", align_bytes=64
+            )
+            regroup(w3_grouped[t][:], w3_raw[t][:])
+            load_w3(t + RAW_TREES)
 
         def quantise_w3(t):
             if live(t):
-                w3_mx[t] = quantise(per_tree, "w3", w3_grouped[t], PASSES * D_OUT)
+                w3_mx[t] = mx_tiles("w3", PASSES * D_OUT)
+                quantise(w3_mx[t], w3_grouped[t], 0, PASSES * D_OUT)
 
         def stage1(t, half):
             if not live(t):
@@ -226,9 +222,9 @@ def tile_randomforestmlp_pa_kernel(tc, h1, W2, b2, W3, b3, out):
                 if c % 2 == 0:
                     bank = h2_psum.tile([P, 2, BATCH], F32, name="h2_bank")
                     h2_banks[t, half, c // 2] = bank
-                m_cols = slice(c * P, (c + 1) * P)
+                m_cols = slice(half * K_PASS + c * P, half * K_PASS + (c + 1) * P)
                 for g in range(PASSES):
-                    w2_codes, w2_scales = w2_units[(t * PASSES + g) * HALVES + half]
+                    w2_codes, w2_scales = w2_mx[t, g]
                     b_cols = slice(g * BATCH, (g + 1) * BATCH)
                     nc.tensor.matmul_mx(
                         out=bank[:, c % 2, :],
@@ -243,13 +239,15 @@ def tile_randomforestmlp_pa_kernel(tc, h1, W2, b2, W3, b3, out):
         def exit_h2(t, half):
             if not live(t):
                 return
-            h2_plain[t, half] = per_half.tile([P, CHUNKS * BATCH], BF16, name="h2_plain")
+            if half == 0:
+                h2_plain[t] = stage.tile([P, HALVES * CHUNKS * BATCH], BF16, name="h2_plain")
             last = t == TREES - 1 and half == HALVES - 1
             for c in range(CHUNKS):
                 column = c * TREES * HALVES + t * HALVES + half
                 bias = b2_columns[:, column : column + 1]
                 sums = h2_banks[t, half, c // 2][:, c % 2, :]
-                rows = h2_plain[t, half][:, c * BATCH : (c + 1) * BATCH]
+                place = half * CHUNKS + c
+                rows = h2_plain[t][:, place * BATCH : (place + 1) * BATCH]
                 if last and c >= CHUNKS // 2:
                     nc.vector.tensor_scalar(
                         out=rows, in0=sums, scalar1=bias, scalar2=0.0, op0=ADD, op1=MAX
@@ -257,41 +255,42 @@ def tile_randomforestmlp_pa_kernel(tc, h1, W2, b2, W3, b3, out):
                 else:
                     nc.scalar.activation(out=rows, in_=sums, func=RELU, bias=bias, scale=1.0)
 
-        def regroup_h2(t, half):
+        def regroup_h2(t, first=0, last=HALVES):
             if not live(t):
                 return
-            h2_grouped[t, half] = per_half.tile(
-                [P, PACK * BATCH], BF16, name="h2_grouped", align_bytes=64
-            )
-            regroup(
-                nc.vector.tensor_copy,
-                h2_grouped[t, half][:],
-                h2_plain[t, half][:].rearrange("p (j b) -> p j b", j=PACK),
-            )
+            if first == 0:
+                h2_grouped[t] = stage.tile(
+                    [P, HALVES * PACK * BATCH], BF16, name="h2_grouped", align_bytes=64
+                )
+            cols = slice(first * PACK * BATCH, last * PACK * BATCH)
+            regroup(h2_grouped[t][:, cols], h2_plain[t][:, cols])
 
-        def quantise_h2(t, half):
-            if live(t):
-                h2_mx[t, half] = quantise(per_half, "h2", h2_grouped[t, half], BATCH)
-
-        def stage2(t, g):
+        def quantise_h2(t, first=0, last=HALVES):
             if not live(t):
                 return
-            h2_codes, h2_scales = h2_mx[t, g]
+            if first == 0:
+                h2_mx[t] = mx_tiles("h2", HALVES * BATCH)
+            quantise(h2_mx[t], h2_grouped[t], first * BATCH, last * BATCH)
+
+        def stage2(t, half):
+            if not live(t):
+                return
+            h2_codes, h2_scales = h2_mx[t]
             w3_codes, w3_scales = w3_mx[t]
-            n_cols = slice(g * D_OUT, (g + 1) * D_OUT)
+            n_cols = slice(half * D_OUT, (half + 1) * D_OUT)
             for r in range(B_TILES):
-                m_cols = slice(r * P, (r + 1) * P)
+                m_cols = slice(half * BATCH + r * P, half * BATCH + (r + 1) * P)
                 nc.tensor.matmul_mx(
                     out=acc[r][:],
                     lhsT=h2_codes[:, m_cols].bitcast(FP8X4),
                     lhsT_scale=h2_scales[:, m_cols],
                     rhs=w3_codes[:, n_cols].bitcast(FP8X4),
                     rhs_scale=w3_scales[:, n_cols],
-                    start=(t == 0 and g == 0),
-                    stop=(t == TREES - 1 and g == PASSES - 1),
+                    start=(t == 0 and half == 0),
+                    stop=(t == TREES - 1 and half == HALVES - 1),
                 )
 
-        b2_rows = const.tile([P, UNIT_COLS], BF16, name="b2_rows")
+        b2_rows = const.tile([P, K_PASS], BF16, name="b2_rows")
         b3_rows = const.tile([P, D_OUT], BF16, name="b3_rows")
         ones = const.tile([P, P], BF16, name="ones")
         nc.vector.memset(b2_rows[:], 0.0)
@@ -303,15 +302,12 @@ def tile_randomforestmlp_pa_kernel(tc, h1, W2, b2, W3, b3, out):
         nc.scalar.dma_start(out=b3_rows[:TREES, :], in_=b3)
         warm = const.tile([P, 1], F32, name="warm")
         nc.scalar.activation(out=warm[:], in_=ones[:, :1], func=RELU)
-        load_w2(0, 0, 0)
-        load_w2(0, 0, 1)
+        load_w2(0, 0)
         load_h1(0)
-        load_w3(0, pieces=PASSES)
-        load_w2(0, 1, 0)
-        load_w2(0, 1, 1)
-        load_w2(1, 0, 0)
+        load_w2(0, 1)
+        load_w3(0)
         load_h1(1)
-        load_w2(1, 0, 1)
+        load_w2(1, 0)
         load_w2(1, 1)
         load_w3(1)
         for t in range(2, RAW_TREES):
@@ -331,7 +327,7 @@ def tile_randomforestmlp_pa_kernel(tc, h1, W2, b2, W3, b3, out):
         b2_banks = []
 
         def prepare_b2_rows():
-            b2_rows_f32 = const.tile([P, UNIT_COLS], F32, name="b2_rows_f32")
+            b2_rows_f32 = const.tile([P, K_PASS], F32, name="b2_rows_f32")
             nc.vector.tensor_copy(
                 out=b2_rows_f32[:].rearrange("p (j m) -> p m j", j=PACK),
                 in_=b2_rows[:].rearrange("p (m j) -> p m j", j=PACK),
@@ -352,66 +348,90 @@ def tile_randomforestmlp_pa_kernel(tc, h1, W2, b2, W3, b3, out):
             nc.tensor.matmul(out=b3_bank[:, 0, :], lhsT=ones[:], rhs=b3_rows[:], start=True, stop=True)
             nc.scalar.mul(out=b3_mean[:], in_=b3_bank[:, 0, :], mul=1.0 / TREES)
 
-        regroup_w2_scalar(0)
-        regroup_w2_vector(0)
-        move_w2(1)
-        transpose_h1(0)
-        regroup_w2_scalar(1)
+        regroup_w2_scalar(0, 0, 0, 1)
+        regroup_w2_vector(0, 0, 0, 1)
+        regroup_w2_scalar(0, 0, 1, 2)
+        regroup_w2_vector(0, 0, 1, 2)
+        transpose_h1(0, 0)
         exit_h1(0, 0)
+        transpose_h1(0, 1)
+        quantise_w2(0, 0, 0, 1)
+        prepare_b2_rows()
+        quantise_w2(0, 0, 1, 2)
+        regroup_w2_scalar(0, 1, 0, 1)
         exit_h1(0, 1)
+        regroup_w2_vector(0, 1, 0, 1)
+        quantise_h1(0)
+        regroup_w2_scalar(0, 1, 1, 2)
+        move_w2(0, 1)
+        regroup_w2_vector(0, 1, 1, 2)
+        exit_w2(0, 1)
+        prepare_b2_columns()
+        quantise_w2(0, 1, 0, 1)
+        stage1(0, 0)
+        quantise_w2(0, 1, 1, 2)
+        stage1(0, 1)
+        transpose_h1(1, 0)
+        move_w2(1, 0)
+        regroup_w3(0)
+        exit_h2(0, 0)
+        exit_h2(0, 1)
+        exit_h1(1, 0)
+        transpose_h1(1, 1)
+        regroup_w2_scalar(1, 0)
+        exit_h1(1, 1)
+        quantise_w3(0)
+        regroup_h2(0)
+        regroup_w2_vector(1, 0)
 
-        for t in range(TREES + 1):
-            first = t * UNITS_PER_TREE
-            exit_w2(first + 1)
-            move_w2(first + 2)
-            regroup_w2_scalar(first + 2)
-            regroup_w2_vector(first + 1)
-            quantise_w2(first)
-            if t == 0:
-                regroup_w3(0, 0)
-                regroup_w3(0, 1)
-                prepare_b2_rows()
-            regroup_h2(t - 1, 0)
-            exit_h2(t - 1, 1)
-            quantise_w3(t - 1)
-
-            exit_w2(first + 2)
-            move_w2(first + 3)
-            regroup_w2_scalar(first + 3)
-            regroup_w2_vector(first + 2)
-            quantise_w2(first + 1)
+        for t in range(1, TREES):
+            exit_w2(t, 0)
+            move_w2(t, 1)
+            transpose_h1(t + 1, 0)
+            regroup_w2_scalar(t, 1)
+            if t > 1:
+                exit_h2(t - 1, 0)
+                exit_h2(t - 1, 1)
+            exit_h1(t + 1, 0)
+            quantise_w2(t, 0)
+            regroup_w2_vector(t, 1)
+            if t > 1:
+                quantise_w3(t - 1)
+                regroup_h2(t - 1)
             quantise_h1(t)
-            if t == 0:
-                prepare_b2_columns()
             if t == 1:
                 prepare_b3()
-            quantise_h2(t - 1, 0)
-            stage2(t - 1, 0)
-            regroup_h2(t - 1, 1)
 
-            exit_w2(first + 3)
-            move_w2(first + 4)
-            regroup_w2_scalar(first + 4)
-            regroup_w2_vector(first + 3)
-            quantise_w2(first + 2)
-            transpose_h1(t + 1)
-            exit_h1(t + 1, 0)
-            stage1(t, 0)
-            quantise_h2(t - 1, 1)
-            stage2(t - 1, 1)
-            if t > 0:
-                regroup_w3(t, 0)
-
-            exit_w2(first + 4)
-            move_w2(first + 5)
-            regroup_w2_scalar(first + 5)
-            exit_h2(t, 0)
+            exit_w2(t, 1)
+            move_w2(t + 1, 0)
+            transpose_h1(t + 1, 1)
+            regroup_w2_scalar(t + 1, 0)
             exit_h1(t + 1, 1)
-            regroup_w2_vector(first + 4)
-            quantise_w2(first + 3)
-            stage1(t, 1)
-            if t > 0:
-                regroup_w3(t, 1)
+            if t < TREES - 1:
+                quantise_w2(t, 1)
+                stage1(t, 0)
+                stage1(t, 1)
+            else:
+                quantise_w2(t, 1, 0, 1)
+                stage1(t, 0)
+                quantise_w2(t, 1, 1, 2)
+                exit_h2(t, 0)
+                stage1(t, 1)
+            regroup_w2_vector(t + 1, 0)
+            quantise_h2(t - 1)
+            stage2(t - 1, 0)
+            stage2(t - 1, 1)
+            regroup_w3(t)
+
+        last = TREES - 1
+        regroup_h2(last, 0, 1)
+        exit_h2(last, 1)
+        quantise_w3(last)
+        quantise_h2(last, 0, 1)
+        stage2(last, 0)
+        regroup_h2(last, 1, 2)
+        quantise_h2(last, 1, 2)
+        stage2(last, 1)
 
         out_rows = const.tile([P, B_TILES, D_OUT], F32, name="out_rows")
         for r in range(B_TILES):

@@ -26,9 +26,9 @@ CHUNKS = K_PASS // P
 HALVES = D_K // K_PASS
 GROUPS = K_PASS // PACK
 
-SCALAR_GROUPS = 48
+SCALAR_GROUPS = 40
 TENSOR_GROUPS = 32
-FIRST_SCALAR_GROUPS = 72
+FIRST_SCALAR_GROUPS = 48
 RUN = 4
 RAW_TREES = 4
 
@@ -90,7 +90,10 @@ def tile_randomforestmlp_pa_kernel(tc, h1, W2, b2, W3, b3, out):
             words = h1_raw[t][:].bitcast(F32).rearrange(
                 "p (r g w u) -> p r g u w", r=B_TILES, g=PASSES, u=2
             )
-            h1_banks[t, g] = tr_psum.tile([P, 2, BATCH], F32, name="h1_bank")
+            if (t, g) == (0, PASSES - 1):
+                h1_banks[t, g] = h2_psum.tile([P, 2, BATCH], F32, name="h1_bank_0", tag="h2_bank")
+            else:
+                h1_banks[t, g] = tr_psum.tile([P, 2, BATCH], F32, name="h1_bank")
             for u in range(2):
                 for r in range(B_TILES):
                     nc.tensor.transpose(
@@ -307,14 +310,14 @@ def tile_randomforestmlp_pa_kernel(tc, h1, W2, b2, W3, b3, out):
         load_w2(0, 1)
         load_w3(0)
         load_h1(1)
+        load_w3(1)
         load_w2(1, 0)
         load_w2(1, 1)
-        load_w3(1)
         for t in range(2, RAW_TREES):
             load_h1(t)
+            load_w3(t)
             for g in range(PASSES):
                 load_w2(t, g)
-            load_w3(t)
         identity = const.tile([P, P], F32, name="identity")
         make_identity(nc, identity[:])
         identity_bf16 = const.tile([P, P], BF16, name="identity_bf16")
@@ -353,33 +356,34 @@ def tile_randomforestmlp_pa_kernel(tc, h1, W2, b2, W3, b3, out):
         regroup_w2_scalar(0, 0, 1, 2)
         regroup_w2_vector(0, 0, 1, 2)
         transpose_h1(0, 0)
-        exit_h1(0, 0)
         transpose_h1(0, 1)
+        exit_h1(0, 0)
+        exit_h1(0, 1)
         quantise_w2(0, 0, 0, 1)
         prepare_b2_rows()
         quantise_w2(0, 0, 1, 2)
         regroup_w2_scalar(0, 1, 0, 1)
-        exit_h1(0, 1)
         regroup_w2_vector(0, 1, 0, 1)
-        quantise_h1(0)
         regroup_w2_scalar(0, 1, 1, 2)
         move_w2(0, 1)
         regroup_w2_vector(0, 1, 1, 2)
+        quantise_h1(0)
         exit_w2(0, 1)
+        transpose_h1(1, 0)
+        exit_h1(1, 0)
         prepare_b2_columns()
         quantise_w2(0, 1, 0, 1)
         stage1(0, 0)
         quantise_w2(0, 1, 1, 2)
         stage1(0, 1)
-        transpose_h1(1, 0)
         move_w2(1, 0)
         regroup_w3(0)
         exit_h2(0, 0)
         exit_h2(0, 1)
-        exit_h1(1, 0)
         transpose_h1(1, 1)
         regroup_w2_scalar(1, 0)
         exit_h1(1, 1)
+        regroup_w3(1)
         quantise_w3(0)
         regroup_h2(0)
         regroup_w2_vector(1, 0)
@@ -395,10 +399,11 @@ def tile_randomforestmlp_pa_kernel(tc, h1, W2, b2, W3, b3, out):
             exit_h1(t + 1, 0)
             quantise_w2(t, 0)
             regroup_w2_vector(t, 1)
-            if t > 1:
-                quantise_w3(t - 1)
-                regroup_h2(t - 1)
+            if t < TREES - 1:
+                quantise_w3(t)
             quantise_h1(t)
+            if t > 1:
+                regroup_h2(t - 1)
             if t == 1:
                 prepare_b3()
 
@@ -421,7 +426,8 @@ def tile_randomforestmlp_pa_kernel(tc, h1, W2, b2, W3, b3, out):
             quantise_h2(t - 1)
             stage2(t - 1, 0)
             stage2(t - 1, 1)
-            regroup_w3(t)
+            if t != TREES - 2:
+                regroup_w3(min(t + 1, TREES - 1))
 
         last = TREES - 1
         regroup_h2(last, 0, 1)

@@ -199,8 +199,8 @@ def tile_randomforestmlp_pa_kernel(tc, h1, W2, b2, W3, b3, out):
 
         def regroup(grouped, rows):
             nc.vector.tensor_copy(
-                out=grouped.rearrange("p (h c i j) -> p h c j i", h=grouped.shape[1] // (PACK * BATCH), i=RUN, j=PACK),
-                in_=rows.rearrange("p (h j c i) -> p h c j i", h=grouped.shape[1] // (PACK * BATCH), j=PACK, i=RUN),
+                out=grouped.rearrange("p (h c i j) -> p h c j i", h=rows.shape[1], i=RUN, j=PACK),
+                in_=rows.rearrange("p h j (c i) -> p h c j i", i=RUN),
             )
 
         def regroup_w3(t):
@@ -209,7 +209,8 @@ def tile_randomforestmlp_pa_kernel(tc, h1, W2, b2, W3, b3, out):
             w3_grouped[t] = stage.tile(
                 [P, PASSES * PACK * D_OUT], BF16, name="w3_grouped", align_bytes=64
             )
-            regroup(w3_grouped[t][:], w3_raw[t][:])
+            rows = w3_raw[t][:].rearrange("p (g j n) -> p g j n", g=PASSES, j=PACK)
+            regroup(w3_grouped[t][:], rows)
             load_w3(t + RAW_TREES)
 
         def quantise_w3(t):
@@ -258,30 +259,33 @@ def tile_randomforestmlp_pa_kernel(tc, h1, W2, b2, W3, b3, out):
                 else:
                     nc.scalar.activation(out=rows, in_=sums, func=RELU, bias=bias, scale=1.0)
 
-        def regroup_h2(t, first=0, last=HALVES):
+        def regroup_h2(t, first=0, last=HALVES, b_first=0, b_last=BATCH):
             if not live(t):
                 return
-            if first == 0:
+            if t not in h2_grouped:
                 h2_grouped[t] = stage.tile(
                     [P, HALVES * PACK * BATCH], BF16, name="h2_grouped", align_bytes=64
                 )
-            cols = slice(first * PACK * BATCH, last * PACK * BATCH)
-            regroup(h2_grouped[t][:, cols], h2_plain[t][:, cols])
+            rows = h2_plain[t][:].rearrange("p (h j b) -> p h j b", h=HALVES, j=PACK)
+            cols = slice(PACK * (first * BATCH + b_first), PACK * ((last - 1) * BATCH + b_last))
+            regroup(h2_grouped[t][:, cols], rows[:, first:last, :, b_first:b_last])
 
-        def quantise_h2(t, first=0, last=HALVES):
+        def quantise_h2(t, first=0, last=HALVES, b_first=0, b_last=BATCH):
             if not live(t):
                 return
-            if first == 0:
+            if t not in h2_mx:
                 h2_mx[t] = mx_tiles("h2", HALVES * BATCH)
-            quantise(h2_mx[t], h2_grouped[t], first * BATCH, last * BATCH)
+            quantise(
+                h2_mx[t], h2_grouped[t], first * BATCH + b_first, (last - 1) * BATCH + b_last
+            )
 
-        def stage2(t, half):
+        def stage2(t, half, sides=range(B_TILES)):
             if not live(t):
                 return
             h2_codes, h2_scales = h2_mx[t]
             w3_codes, w3_scales = w3_mx[t]
             n_cols = slice(half * D_OUT, (half + 1) * D_OUT)
-            for r in range(B_TILES):
+            for r in sides:
                 m_cols = slice(half * BATCH + r * P, half * BATCH + (r + 1) * P)
                 nc.tensor.matmul_mx(
                     out=acc[r][:],
@@ -396,7 +400,6 @@ def tile_randomforestmlp_pa_kernel(tc, h1, W2, b2, W3, b3, out):
             if t > 1:
                 exit_h2(t - 1, 0)
                 exit_h2(t - 1, 1)
-            exit_h1(t + 1, 0)
             quantise_w2(t, 0)
             regroup_w2_vector(t, 1)
             if t < TREES - 1:
@@ -408,6 +411,7 @@ def tile_randomforestmlp_pa_kernel(tc, h1, W2, b2, W3, b3, out):
                 prepare_b3()
 
             exit_w2(t, 1)
+            exit_h1(t + 1, 0)
             move_w2(t + 1, 0)
             transpose_h1(t + 1, 1)
             regroup_w2_scalar(t + 1, 0)
@@ -435,9 +439,11 @@ def tile_randomforestmlp_pa_kernel(tc, h1, W2, b2, W3, b3, out):
         quantise_w3(last)
         quantise_h2(last, 0, 1)
         stage2(last, 0)
-        regroup_h2(last, 1, 2)
-        quantise_h2(last, 1, 2)
-        stage2(last, 1)
+        for r in range(B_TILES):
+            regroup_h2(last, 1, 2, r * P, (r + 1) * P)
+        for r in range(B_TILES):
+            quantise_h2(last, 1, 2, r * P, (r + 1) * P)
+            stage2(last, 1, [r])
 
         out_rows = const.tile([P, B_TILES, D_OUT], F32, name="out_rows")
         for r in range(B_TILES):

@@ -364,20 +364,20 @@ def tile_randomforestmlp_pa_kernel(tc, h1, W2, b2, W3, b3, out):
         exit_h1(0, 0)
         exit_h1(0, 1)
         quantise_w2(0, 0, 0, 1)
-        prepare_b2_rows()
         quantise_w2(0, 0, 1, 2)
         regroup_w2_scalar(0, 1, 0, 1)
         regroup_w2_vector(0, 1, 0, 1)
         regroup_w2_scalar(0, 1, 1, 2)
         move_w2(0, 1)
         regroup_w2_vector(0, 1, 1, 2)
+        prepare_b2_rows()
         quantise_h1(0)
         exit_w2(0, 1)
         transpose_h1(1, 0)
         exit_h1(1, 0)
-        prepare_b2_columns()
         quantise_w2(0, 1, 0, 1)
         stage1(0, 0)
+        prepare_b2_columns()
         quantise_w2(0, 1, 1, 2)
         stage1(0, 1)
         move_w2(1, 0)
@@ -445,14 +445,17 @@ def tile_randomforestmlp_pa_kernel(tc, h1, W2, b2, W3, b3, out):
             quantise_h2(last, 1, 2, r * P, (r + 1) * P)
             stage2(last, 1, [r])
 
-        out_rows = const.tile([P, B_TILES, D_OUT], F32, name="out_rows")
+        stores = (nc.sync, nc.scalar)
         for r in range(B_TILES):
+            out_rows = const.tile([P, D_OUT], F32, name="out_rows%d" % r)
             nc.vector.scalar_tensor_tensor(
-                out=out_rows[:, r, :],
+                out=out_rows[:],
                 in0=acc[r][:],
                 scalar=1.0 / TREES,
                 in1=b3_mean[:],
                 op0=MULT,
                 op1=ADD,
             )
-        nc.sync.dma_start(out=out.rearrange("(p r) n -> p r n", r=B_TILES), in_=out_rows[:])
+            stores[r].dma_start(
+                out=out.rearrange("(p r) n -> p r n", r=B_TILES)[:, r, :], in_=out_rows[:]
+            )

@@ -26,7 +26,7 @@ CHUNKS = K_PASS // P
 HALVES = D_K // K_PASS
 GROUPS = K_PASS // PACK
 
-SCALAR_GROUPS = 40
+SCALAR_GROUPS = 44
 TENSOR_GROUPS = 32
 FIRST_SCALAR_GROUPS = 48
 RUN = 4
@@ -152,9 +152,16 @@ def tile_randomforestmlp_pa_kernel(tc, h1, W2, b2, W3, b3, out):
         def regroup_w2_scalar(t, g, first=0, last=HALVES):
             if not live(t):
                 return
-            source, target = w2_views(t, g)
-            stop = shares(t, g)[0]
-            nc.scalar.copy(out=target[:, first:last, :stop], in_=source[:, first:last, :stop])
+            w2_views(t, g)
+            stop = shares(t, g)[0] // 2
+            source = w2_raw[t, g][:].rearrange(
+                "p (j h m r i) -> p h m j r i", j=PACK, h=HALVES, r=2, i=PACK
+            )
+            target = w2_grouped[t, g][:].rearrange(
+                "p (h i m r j) -> p h m j r i", h=HALVES, i=PACK, r=2, j=PACK
+            )
+            for half in range(first, last):
+                nc.scalar.copy(out=target[:, half, :stop], in_=source[:, half, :stop])
 
         def regroup_w2_vector(t, g, first=0, last=HALVES):
             if not live(t):

@@ -29,7 +29,7 @@ GROUPS = K_PASS // PACK
 SCALAR_GROUPS = 44
 TENSOR_GROUPS = 32
 FIRST_SCALAR_GROUPS = 48
-RUN = 4
+RUN = 8
 RAW_TREES = 4
 
 
@@ -204,21 +204,24 @@ def tile_randomforestmlp_pa_kernel(tc, h1, W2, b2, W3, b3, out):
                 w2_mx[t, g] = mx_tiles("w2", D_K)
             quantise(w2_mx[t, g], w2_grouped[t, g], first * K_PASS, last * K_PASS)
 
-        def regroup(grouped, rows):
-            nc.vector.tensor_copy(
+        def regroup(copy, grouped, rows):
+            copy(
                 out=grouped.rearrange("p (h c i j) -> p h c j i", h=rows.shape[1], i=RUN, j=PACK),
                 in_=rows.rearrange("p h j (c i) -> p h c j i", i=RUN),
             )
 
-        def regroup_w3(t):
+        def regroup_w3(t, copy=nc.vector.tensor_copy, first=0, last=PASSES):
             if not live(t):
                 return
-            w3_grouped[t] = stage.tile(
-                [P, PASSES * PACK * D_OUT], BF16, name="w3_grouped", align_bytes=64
-            )
+            if t not in w3_grouped:
+                w3_grouped[t] = stage.tile(
+                    [P, PASSES * PACK * D_OUT], BF16, name="w3_grouped", align_bytes=64
+                )
             rows = w3_raw[t][:].rearrange("p (g j n) -> p g j n", g=PASSES, j=PACK)
-            regroup(w3_grouped[t][:], rows)
-            load_w3(t + RAW_TREES)
+            cols = slice(first * PACK * D_OUT, last * PACK * D_OUT)
+            regroup(copy, w3_grouped[t][:, cols], rows[:, first:last])
+            if last == PASSES:
+                load_w3(t + RAW_TREES)
 
         def quantise_w3(t):
             if live(t):
@@ -275,7 +278,7 @@ def tile_randomforestmlp_pa_kernel(tc, h1, W2, b2, W3, b3, out):
                 )
             rows = h2_plain[t][:].rearrange("p (h j b) -> p h j b", h=HALVES, j=PACK)
             cols = slice(PACK * (first * BATCH + b_first), PACK * ((last - 1) * BATCH + b_last))
-            regroup(h2_grouped[t][:, cols], rows[:, first:last, :, b_first:b_last])
+            regroup(nc.vector.tensor_copy, h2_grouped[t][:, cols], rows[:, first:last, :, b_first:b_last])
 
         def quantise_h2(t, first=0, last=HALVES, b_first=0, b_last=BATCH):
             if not live(t):
@@ -326,9 +329,9 @@ def tile_randomforestmlp_pa_kernel(tc, h1, W2, b2, W3, b3, out):
         load_w2(1, 1)
         for t in range(2, RAW_TREES):
             load_h1(t)
+            load_w2(t, 0)
             load_w3(t)
-            for g in range(PASSES):
-                load_w2(t, g)
+            load_w2(t, 1)
         identity = const.tile([P, P], F32, name="identity")
         make_identity(nc, identity[:])
         identity_bf16 = const.tile([P, P], BF16, name="identity_bf16")
@@ -403,10 +406,10 @@ def tile_randomforestmlp_pa_kernel(tc, h1, W2, b2, W3, b3, out):
             exit_w2(t, 0)
             move_w2(t, 1)
             transpose_h1(t + 1, 0)
-            regroup_w2_scalar(t, 1)
             if t > 1:
                 exit_h2(t - 1, 0)
                 exit_h2(t - 1, 1)
+            regroup_w2_scalar(t, 1)
             quantise_w2(t, 0)
             regroup_w2_vector(t, 1)
             if t < TREES - 1:
@@ -428,6 +431,7 @@ def tile_randomforestmlp_pa_kernel(tc, h1, W2, b2, W3, b3, out):
                 stage1(t, 0)
                 stage1(t, 1)
             else:
+                regroup_w3(t, nc.scalar.copy, first=1, last=2)
                 quantise_w2(t, 1, 0, 1)
                 stage1(t, 0)
                 quantise_w2(t, 1, 1, 2)
@@ -437,8 +441,10 @@ def tile_randomforestmlp_pa_kernel(tc, h1, W2, b2, W3, b3, out):
             quantise_h2(t - 1)
             stage2(t - 1, 0)
             stage2(t - 1, 1)
-            if t != TREES - 2:
-                regroup_w3(min(t + 1, TREES - 1))
+            if t < TREES - 2:
+                regroup_w3(t + 1)
+            elif t == TREES - 1:
+                regroup_w3(t, first=0, last=1)
 
         last = TREES - 1
         regroup_h2(last, 0, 1)

@@ -26,7 +26,7 @@ CHUNKS = K_PASS // P
 HALVES = D_K // K_PASS
 GROUPS = K_PASS // PACK
 
-SCALAR_GROUPS = 44
+SCALAR_GROUPS = 48
 TENSOR_GROUPS = 32
 FIRST_SCALAR_GROUPS = 48
 RUN = 8
@@ -427,8 +427,9 @@ def tile_randomforestmlp_pa_kernel(tc, h1, W2, b2, W3, b3, out):
             regroup_w2_scalar(t + 1, 0)
             exit_h1(t + 1, 1)
             if t < TREES - 1:
-                quantise_w2(t, 1)
+                quantise_w2(t, 1, 0, 1)
                 stage1(t, 0)
+                quantise_w2(t, 1, 1, 2)
                 stage1(t, 1)
             else:
                 regroup_w3(t, nc.scalar.copy, first=1, last=2)
@@ -458,17 +459,14 @@ def tile_randomforestmlp_pa_kernel(tc, h1, W2, b2, W3, b3, out):
             quantise_h2(last, 1, 2, r * P, (r + 1) * P)
             stage2(last, 1, [r])
 
-        stores = (nc.sync, nc.scalar)
+        out_rows = const.tile([P, B_TILES, D_OUT], F32, name="out_rows")
         for r in range(B_TILES):
-            out_rows = const.tile([P, D_OUT], F32, name="out_rows%d" % r)
             nc.vector.scalar_tensor_tensor(
-                out=out_rows[:],
+                out=out_rows[:, r, :],
                 in0=acc[r][:],
                 scalar=1.0 / TREES,
                 in1=b3_mean[:],
                 op0=MULT,
                 op1=ADD,
             )
-            stores[r].dma_start(
-                out=out.rearrange("(p r) n -> p r n", r=B_TILES)[:, r, :], in_=out_rows[:]
-            )
+        nc.sync.dma_start(out=out.rearrange("(p r) n -> p r n", r=B_TILES), in_=out_rows[:])

from contextlib import ExitStack

import concourse.mybir as mybir
from concourse.masks import make_identity

BF16 = mybir.dt.bfloat16
F32 = mybir.dt.float32
U32 = mybir.dt.uint32
U8 = mybir.dt.uint8
FP8X4 = mybir.dt.float8_e4m3fn_x4
RELU = mybir.ActivationFunctionType.Relu
MULT = mybir.AluOpType.mult
ADD = mybir.AluOpType.add
MAX = mybir.AluOpType.max

TREES, BATCH, D_H, D_K, D_OUT = 8, 256, 1024, 1024, 256
FLOPS = 2 * TREES * BATCH * (D_H * D_K + D_K * D_OUT)

P = 128
PACK = 4
K_PASS = P * PACK
PASSES = D_H // K_PASS
B_TILES = BATCH // P
CHUNKS = K_PASS // P

HALVES = D_K // K_PASS
GROUPS = K_PASS // PACK

SCALAR_GROUPS = 48
TENSOR_GROUPS = 32
FIRST_SCALAR_GROUPS = 48
RUN = 8
RAW_TREES = 4


def tile_randomforestmlp_pa_kernel(tc, h1, W2, b2, W3, b3, out):
    nc = tc.nc
    with ExitStack() as ctx:
        const = ctx.enter_context(tc.tile_pool(name="const", bufs=1))
        raw = ctx.enter_context(tc.tile_pool(name="raw", bufs=RAW_TREES))
        stage = ctx.enter_context(tc.tile_pool(name="stage", bufs=3))
        mx = ctx.enter_context(tc.tile_pool(name="mx", bufs=4))
        acc_psum = ctx.enter_context(tc.psum_pool(name="acc_psum", bufs=1))
        tr_psum = ctx.enter_context(tc.psum_pool(name="tr_psum", bufs=1))
        mv_psum = ctx.enter_context(tc.psum_pool(name="mv_psum", bufs=1))
        h2_psum = ctx.enter_context(tc.psum_pool(name="h2_psum", bufs=4))
        ctx.enter_context(tc.manual_schedule())

        h1_raw, w2_raw, w3_raw = {}, {}, {}
        h1_banks, h1_grouped, h1_mx = {}, {}, {}
        w2_banks, w2_grouped, w2_mx = {}, {}, {}
        w3_grouped, w3_mx = {}, {}
        h2_banks, h2_plain, h2_grouped, h2_mx = {}, {}, {}, {}

        def live(t):
            return 0 <= t < TREES

        def load_h1(t):
            if not live(t):
                return
            h1_raw[t] = raw.tile([P, B_TILES * D_H], BF16, name="h1_raw")
            nc.sync.dma_start(
                out=h1_raw[t][:], in_=h1[t].rearrange("(p r) k -> p (r k)", r=B_TILES)
            )

        def load_w2(t, g, half=None):
            if not live(t):
                return
            if (t, g) not in w2_raw:
                w2_raw[t, g] = raw.tile([P, PACK * D_K], BF16, name="w2_raw%d" % g)
            cols = slice(0, D_K) if half is None else slice(half * K_PASS, (half + 1) * K_PASS)
            rows = W2[t, g * K_PASS : (g + 1) * K_PASS, :].rearrange("(p j) n -> p j n", j=PACK)
            nc.sync.dma_start(
                out=w2_raw[t, g][:].rearrange("p (j n) -> p j n", j=PACK)[:, :, cols],
                in_=rows[:, :, cols],
            )

        def load_w3(t):
            if not live(t):
                return
            w3_raw[t] = raw.tile([P, PASSES * PACK * D_OUT], BF16, name="w3_raw")
            nc.sync.dma_start(
                out=w3_raw[t][:].rearrange("p (g x) -> p g x", g=PASSES),
                in_=W3[t].rearrange("(g p j) n -> p g (j n)", p=P, j=PACK),
            )

        def transpose_h1(t, g):
            if not live(t):
                return
            words = h1_raw[t][:].bitcast(F32).rearrange(
                "p (r g w u) -> p r g u w", r=B_TILES, g=PASSES, u=2
            )
            if (t, g) == (0, PASSES - 1):
                h1_banks[t, g] = h2_psum.tile([P, 2, BATCH], F32, name="h1_bank_0", tag="h2_bank")
            else:
                h1_banks[t, g] = tr_psum.tile([P, 2, BATCH], F32, name="h1_bank")
            for u in range(2):
                for r in range(B_TILES):
                    nc.tensor.transpose(
                        h1_banks[t, g][:, u, r * P : (r + 1) * P], words[:, r, g, u, :], identity[:]
                    )
            if g == PASSES - 1:
                load_h1(t + RAW_TREES)

        def exit_h1(t, g):
            if not live(t):
                return
            if g == 0:
                h1_grouped[t] = stage.tile(
                    [P, PASSES * PACK * BATCH], BF16, name="h1_grouped", align_bytes=64
                )
            one_pass = h1_grouped[t][:, g * PACK * BATCH : (g + 1) * PACK * BATCH]
            nc.scalar.copy(
                out=one_pass.bitcast(F32).rearrange("p (b u) -> p b u", u=2),
                in_=h1_banks[t, g][:].rearrange("p u b -> p b u"),
            )

        def mx_tiles(name, width):
            codes = mx.tile([P, width], U32, name=name + "_codes", align_bytes=64)
            scales = mx.tile([P, width], U8, name=name + "_scales", align_bytes=64)
            return codes, scales

        def quantise(tiles, grouped, first, last):
            codes, scales = tiles
            nc.vector.quantize_mx(
                out=codes[:, first:last].bitcast(FP8X4),
                scales=scales[:, first:last],
                in_=grouped[:, PACK * first : PACK * last],
            )

        def quantise_h1(t):
            if live(t):
                h1_mx[t] = mx_tiles("h1", PASSES * BATCH)
                quantise(h1_mx[t], h1_grouped[t], 0, PASSES * BATCH)

        def w2_views(t, g):
            if (t, g) not in w2_grouped:
                w2_grouped[t, g] = stage.tile(
                    [P, PACK * D_K], BF16, name="w2_grouped", align_bytes=64
                )
            source = w2_raw[t, g][:].rearrange("p (j h m i) -> p h m j i", j=PACK, h=HALVES, i=PACK)
            target = w2_grouped[t, g][:].rearrange(
                "p (h i m j) -> p h m j i", h=HALVES, i=PACK, j=PACK
            )
            return source, target

        def shares(t, g):
            if (t, g) == (0, 0):
                return FIRST_SCALAR_GROUPS, FIRST_SCALAR_GROUPS
            return SCALAR_GROUPS, SCALAR_GROUPS + TENSOR_GROUPS

        def regroup_w2_scalar(t, g, first=0, last=HALVES):
            if not live(t):
                return
            w2_views(t, g)
            stop = shares(t, g)[0] // 2
            source = w2_raw[t, g][:].rearrange(
                "p (j h m r i) -> p h m j r i", j=PACK, h=HALVES, r=2, i=PACK
            )
            target = w2_grouped[t, g][:].rearrange(
                "p (h i m r j) -> p h m j r i", h=HALVES, i=PACK, r=2, j=PACK
            )
            for half in range(first, last):
                nc.scalar.copy(out=target[:, half, :stop], in_=source[:, half, :stop])

        def regroup_w2_vector(t, g, first=0, last=HALVES):
            if not live(t):
                return
            source, target = w2_views(t, g)
            start = shares(t, g)[1]
            nc.vector.tensor_copy(out=target[:, first:last, start:], in_=source[:, first:last, start:])
            if last == HALVES:
                load_w2(t + RAW_TREES, g)

        def move_w2(t, g):
            start, stop = shares(t, g) if live(t) else (0, 0)
            if start == stop:
                return
            source = w2_views(t, g)[0]
            w2_banks[t, g] = mv_psum.tile([P, HALVES, PACK, TENSOR_GROUPS, PACK], BF16, name="w2_bank")
            for half in range(HALVES):
                nc.tensor.matmul(
                    out=w2_banks[t, g][:, half].rearrange("p i m j -> p j m i"),
                    lhsT=identity_bf16[:],
                    rhs=source[:, half, start:stop].rearrange("p m j i -> p j m i"),
                    start=True,
                    stop=True,
                )

        def exit_w2(t, g):
            if (t, g) not in w2_banks:
                return
            start, stop = shares(t, g)
            blocks = w2_grouped[t, g][:].rearrange("p (b x) -> p b x", b=HALVES * PACK)
            nc.scalar.copy(
                out=blocks[:, :, PACK * start : PACK * stop],
                in_=w2_banks[t, g][:].rearrange("p h i m j -> p (h i) (m j)"),
            )

        def quantise_w2(t, g, first=0, last=HALVES):
            if not live(t):
                return
            if first == 0:
                w2_mx[t, g] = mx_tiles("w2", D_K)
            quantise(w2_mx[t, g], w2_grouped[t, g], first * K_PASS, last * K_PASS)

        def regroup(copy, grouped, rows):
            copy(
                out=grouped.rearrange("p (h c i j) -> p h c j i", h=rows.shape[1], i=RUN, j=PACK),
                in_=rows.rearrange("p h j (c i) -> p h c j i", i=RUN),
            )

        def regroup_w3(t, copy=nc.vector.tensor_copy, first=0, last=PASSES):
            if not live(t):
                return
            if t not in w3_grouped:
                w3_grouped[t] = stage.tile(
                    [P, PASSES * PACK * D_OUT], BF16, name="w3_grouped", align_bytes=64
                )
            rows = w3_raw[t][:].rearrange("p (g j n) -> p g j n", g=PASSES, j=PACK)
            cols = slice(first * PACK * D_OUT, last * PACK * D_OUT)
            regroup(copy, w3_grouped[t][:, cols], rows[:, first:last])
            if last == PASSES:
                load_w3(t + RAW_TREES)

        def quantise_w3(t):
            if live(t):
                w3_mx[t] = mx_tiles("w3", PASSES * D_OUT)
                quantise(w3_mx[t], w3_grouped[t], 0, PASSES * D_OUT)

        def stage1(t, half):
            if not live(t):
                return
            h1_codes, h1_scales = h1_mx[t]
            for c in range(CHUNKS):
                if c % 2 == 0:
                    bank = h2_psum.tile([P, 2, BATCH], F32, name="h2_bank")
                    h2_banks[t, half, c // 2] = bank
                m_cols = slice(half * K_PASS + c * P, half * K_PASS + (c + 1) * P)
                for g in range(PASSES):
                    w2_codes, w2_scales = w2_mx[t, g]
                    b_cols = slice(g * BATCH, (g + 1) * BATCH)
                    nc.tensor.matmul_mx(
                        out=bank[:, c % 2, :],
                        lhsT=w2_codes[:, m_cols].bitcast(FP8X4),
                        lhsT_scale=w2_scales[:, m_cols],
                        rhs=h1_codes[:, b_cols].bitcast(FP8X4),
                        rhs_scale=h1_scales[:, b_cols],
                        start=(g == 0),
                        stop=(g == PASSES - 1),
                    )

        def exit_h2(t, half):
            if not live(t):
                return
            if half == 0:
                h2_plain[t] = stage.tile([P, HALVES * CHUNKS * BATCH], BF16, name="h2_plain")
            last = t == TREES - 1 and half == HALVES - 1
            for c in range(CHUNKS):
                column = c * TREES * HALVES + t * HALVES + half
                bias = b2_columns[:, column : column + 1]
                sums = h2_banks[t, half, c // 2][:, c % 2, :]
                place = half * CHUNKS + c
                rows = h2_plain[t][:, place * BATCH : (place + 1) * BATCH]
                if last and c >= CHUNKS // 2:
                    nc.vector.tensor_scalar(
                        out=rows, in0=sums, scalar1=bias, scalar2=0.0, op0=ADD, op1=MAX
                    )
                else:
                    nc.scalar.activation(out=rows, in_=sums, func=RELU, bias=bias, scale=1.0)

        def regroup_h2(t, first=0, last=HALVES, b_first=0, b_last=BATCH):
            if not live(t):
                return
            if t not in h2_grouped:
                h2_grouped[t] = stage.tile(
                    [P, HALVES * PACK * BATCH], BF16, name="h2_grouped", align_bytes=64
                )
            rows = h2_plain[t][:].rearrange("p (h j b) -> p h j b", h=HALVES, j=PACK)
            cols = slice(PACK * (first * BATCH + b_first), PACK * ((last - 1) * BATCH + b_last))
            regroup(nc.vector.tensor_copy, h2_grouped[t][:, cols], rows[:, first:last, :, b_first:b_last])

        def quantise_h2(t, first=0, last=HALVES, b_first=0, b_last=BATCH):
            if not live(t):
                return
            if t not in h2_mx:
                h2_mx[t] = mx_tiles("h2", HALVES * BATCH)
            quantise(
                h2_mx[t], h2_grouped[t], first * BATCH + b_first, (last - 1) * BATCH + b_last
            )

        def stage2(t, half, sides=range(B_TILES)):
            if not live(t):
                return
            h2_codes, h2_scales = h2_mx[t]
            w3_codes, w3_scales = w3_mx[t]
            n_cols = slice(half * D_OUT, (half + 1) * D_OUT)
            for r in sides:
                m_cols = slice(half * BATCH + r * P, half * BATCH + (r + 1) * P)
                nc.tensor.matmul_mx(
                    out=acc[r][:],
                    lhsT=h2_codes[:, m_cols].bitcast(FP8X4),
                    lhsT_scale=h2_scales[:, m_cols],
                    rhs=w3_codes[:, n_cols].bitcast(FP8X4),
                    rhs_scale=w3_scales[:, n_cols],
                    start=(t == 0 and half == 0),
                    stop=(t == TREES - 1 and half == HALVES - 1),
                )

        b2_rows = const.tile([P, K_PASS], BF16, name="b2_rows")
        b3_rows = const.tile([P, D_OUT], BF16, name="b3_rows")
        ones = const.tile([P, P], BF16, name="ones")
        nc.vector.memset(b2_rows[:], 0.0)
        nc.vector.memset(b3_rows[:], 0.0)
        nc.vector.memset(ones[:], 1.0)
        nc.scalar.dma_start(
            out=b2_rows[: TREES * HALVES, :], in_=b2.rearrange("t (h n) -> (t h) n", h=HALVES)
        )
        nc.scalar.dma_start(out=b3_rows[:TREES, :], in_=b3)
        warm = const.tile([P, 1], F32, name="warm")
        nc.scalar.activation(out=warm[:], in_=ones[:, :1], func=RELU)
        load_w2(0, 0)
        load_h1(0)
        load_w2(0, 1)
        load_w3(0)
        load_h1(1)
        load_w3(1)
        load_w2(1, 0)
        load_w2(1, 1)
        for t in range(2, RAW_TREES):
            load_h1(t)
            load_w2(t, 0)
            load_w3(t)
            load_w2(t, 1)
        identity = const.tile([P, P], F32, name="identity")
        make_identity(nc, identity[:])
        identity_bf16 = const.tile([P, P], BF16, name="identity_bf16")
        make_identity(nc, identity_bf16[:])
        acc = [acc_psum.tile([P, D_OUT], F32, name="acc%d" % r) for r in range(B_TILES)]

        b2_columns = const.tile([P, PACK * TREES * HALVES], F32, name="b2_columns")
        b3_mean = const.tile([P, D_OUT], F32, name="b3_mean")

        b2_banks = []

        def prepare_b2_rows():
            b2_rows_f32 = const.tile([P, K_PASS], F32, name="b2_rows_f32")
            nc.vector.tensor_copy(
                out=b2_rows_f32[:].rearrange("p (j m) -> p m j", j=PACK),
                in_=b2_rows[:].rearrange("p (m j) -> p m j", j=PACK),
            )
            b2_bank = h2_psum.tile([P, PACK, P], F32, name="b2_bank", tag="h2_bank")
            for j in range(PACK):
                nc.tensor.transpose(b2_bank[:, j, :], b2_rows_f32[:, j * P : (j + 1) * P], identity[:])
            b2_banks.append(b2_bank)

        def prepare_b2_columns():
            nc.vector.tensor_copy(
                out=b2_columns[:].rearrange("p (j r) -> p j r", j=PACK),
                in_=b2_banks[0][:, :, : TREES * HALVES],
            )

        def prepare_b3():
            b3_bank = h2_psum.tile([P, 2, BATCH], F32, name="b3_bank", tag="h2_bank")
            nc.tensor.matmul(out=b3_bank[:, 0, :], lhsT=ones[:], rhs=b3_rows[:], start=True, stop=True)
            nc.scalar.mul(out=b3_mean[:], in_=b3_bank[:, 0, :], mul=1.0 / TREES)

        regroup_w2_scalar(0, 0, 0, 1)
        regroup_w2_vector(0, 0, 0, 1)
        regroup_w2_scalar(0, 0, 1, 2)
        regroup_w2_vector(0, 0, 1, 2)
        transpose_h1(0, 0)
        transpose_h1(0, 1)
        exit_h1(0, 0)
        exit_h1(0, 1)
        quantise_w2(0, 0, 0, 1)
        quantise_w2(0, 0, 1, 2)
        regroup_w2_scalar(0, 1, 0, 1)
        regroup_w2_vector(0, 1, 0, 1)
        regroup_w2_scalar(0, 1, 1, 2)
        move_w2(0, 1)
        regroup_w2_vector(0, 1, 1, 2)
        prepare_b2_rows()
        quantise_h1(0)
        exit_w2(0, 1)
        transpose_h1(1, 0)
        exit_h1(1, 0)
        quantise_w2(0, 1, 0, 1)
        stage1(0, 0)
        prepare_b2_columns()
        quantise_w2(0, 1, 1, 2)
        stage1(0, 1)
        move_w2(1, 0)
        regroup_w3(0)
        exit_h2(0, 0)
        exit_h2(0, 1)
        transpose_h1(1, 1)
        regroup_w2_scalar(1, 0)
        exit_h1(1, 1)
        regroup_w3(1)
        quantise_w3(0)
        regroup_h2(0)
        regroup_w2_vector(1, 0)

        for t in range(1, TREES):
            exit_w2(t, 0)
            move_w2(t, 1)
            transpose_h1(t + 1, 0)
            if t > 1:
                exit_h2(t - 1, 0)
                exit_h2(t - 1, 1)
            regroup_w2_scalar(t, 1)
            quantise_w2(t, 0)
            regroup_w2_vector(t, 1)
            if t < TREES - 1:
                quantise_w3(t)
            quantise_h1(t)
            if t > 1:
                regroup_h2(t - 1)
            if t == 1:
                prepare_b3()

            exit_w2(t, 1)
            exit_h1(t + 1, 0)
            move_w2(t + 1, 0)
            transpose_h1(t + 1, 1)
            regroup_w2_scalar(t + 1, 0)
            exit_h1(t + 1, 1)
            if t < TREES - 1:
                quantise_w2(t, 1, 0, 1)
                stage1(t, 0)
                quantise_w2(t, 1, 1, 2)
                stage1(t, 1)
            else:
                regroup_w3(t, nc.scalar.copy, first=1, last=2)
                quantise_w2(t, 1, 0, 1)
                stage1(t, 0)
                quantise_w2(t, 1, 1, 2)
                exit_h2(t, 0)
                stage1(t, 1)
            regroup_w2_vector(t + 1, 0)
            quantise_h2(t - 1)
            stage2(t - 1, 0)
            stage2(t - 1, 1)
            if t < TREES - 2:
                regroup_w3(t + 1)
            elif t == TREES - 1:
                regroup_w3(t, first=0, last=1)

        last = TREES - 1
        regroup_h2(last, 0, 1)
        exit_h2(last, 1)
        quantise_w3(last)
        quantise_h2(last, 0, 1)
        stage2(last, 0)
        for r in range(B_TILES):
            regroup_h2(last, 1, 2, r * P, (r + 1) * P)
        for r in range(B_TILES):
            quantise_h2(last, 1, 2, r * P, (r + 1) * P)
            stage2(last, 1, [r])

        out_rows = const.tile([P, B_TILES, D_OUT], F32, name="out_rows")
        for r in range(B_TILES):
            nc.vector.scalar_tensor_tensor(
                out=out_rows[:, r, :],
                in0=acc[r][:],
                scalar=1.0 / TREES,
                in1=b3_mean[:],
                op0=MULT,
                op1=ADD,
            )
        nc.sync.dma_start(out=out.rearrange("(p r) n -> p r n", r=B_TILES), in_=out_rows[:])
